import numpy as np
import ml_dtypes


def mxq(x, axis, fmt="e4m3"):
    dtype, down = {"e4m3": (ml_dtypes.float8_e4m3fn, 7), "e5m2": (ml_dtypes.float8_e5m2, 14)}[fmt]
    v = np.moveaxis(np.asarray(x, np.float32).astype(ml_dtypes.bfloat16).astype(np.float64), axis, -1)
    blocks = v.reshape(v.shape[:-1] + (-1, 32))
    amax = np.abs(blocks).max(-1, keepdims=True)
    byte = np.maximum(np.where(amax > 0, np.frexp(amax)[1] - 1 + 127, 0) - down, 1)
    scale = np.exp2(byte - 127.0)
    codes = (blocks / scale).astype(np.float32).astype(dtype).astype(np.float64)
    return np.moveaxis((codes * scale).reshape(v.shape), -1, axis)


WIDE = False


def mx_kscale(k):
    if not WIDE:
        return np.ones(k)
    levels = np.array([10, -10, 5, -5, 0])
    a = np.random.permutation(np.resize(levels, k // 512 * 4)).reshape(k // 512, 4)
    idx = np.arange(k)
    return np.exp2(a[idx // 512, idx % 128 // 32])


BF16 = ml_dtypes.bfloat16


def bf(x):
    return np.asarray(x, np.float32).astype(BF16)


def f64(x):
    return np.asarray(x).astype(np.float64)


B, T, N, M, D, F = 2, 8, 32, 32, 128, 512
K = 4 * D


def silu(x):
    return x / (1.0 + np.exp(-x))


def setup_inputs():
    s = mx_kscale(K)[:D]
    return {
        "p": bf(np.random.standard_normal((B, T, N, D)) * s),
        "v": bf(np.random.standard_normal((B, T, M, D)) * s),
        "W1": bf(np.random.standard_normal((K, F)) * 0.9 / np.sqrt(K) / np.concatenate([s, s, s * s, s])[:, None]),
        "b1": bf(np.random.standard_normal(F) * 0.3),
        "W2": bf(np.random.standard_normal((F, D)) * 1.5 / np.sqrt(F)),
        "b2": bf(np.random.standard_normal(D) * 0.3),
    }


def reference(p, v, W1, b1, W2, b2):
    p4 = f64(p)[:, :, :, None, :]
    v4 = f64(v)[:, :, None, :, :]
    prod = p4 * v4
    absdiff = np.abs(p4 - v4)
    full = prod.shape
    pair = np.concatenate([np.broadcast_to(p4, full), np.broadcast_to(v4, full), prod, absdiff], axis=-1)
    h = silu((mxq(pair, 4, "e4m3") @ mxq(f64(W1), 0, "e4m3")) + f64(b1))
    grid = (mxq(h, 4, "e4m3") @ mxq(f64(W2), 0, "e4m3")) + f64(b2)
    return grid.reshape(B, T, N * M, D)

@@ -1,0 +1,228 @@
+from contextlib import ExitStack
+
+import concourse.mybir as mybir
+
+BF16 = mybir.dt.bfloat16
+F32 = mybir.dt.float32
+I32 = mybir.dt.int32
+U8 = mybir.dt.uint8
+FP8X4 = mybir.dt.float8_e4m3fn_x4
+ALU = mybir.AluOpType
+ACT = mybir.ActivationFunctionType
+
+P = 128
+PACK = 4
+QUAD = 32
+GRIDS = 16
+N = 32
+M = 32
+D = 128
+F = 512
+GROUPS = 4
+LANES = 4
+BATCHES = GRIDS // LANES
+PAIRS = N * M
+CHUNK = 512
+CHUNKS = PAIRS // CHUNK
+F_TILES = F // P
+ROW_TILES = CHUNK // P
+REPEAT = 4
+
+PLANE = PAIRS // 4
+PACKED = PAIRS + PLANE
+
+FLOPS = 2 * GRIDS * PAIRS * (GROUPS * D * F + F * D)
+
+
+def words_of(packed, first, count):
+    return packed[:, first : first + count].bitcast(FP8X4)
+
+
+def scales_of(packed, words, first, count):
+    return packed[:, words + first // 4 : words + (first + count) // 4].bitcast(U8)
+
+
+def tile_pairinteractiongrid_pa_t_kernel(tc, p, v, W1, b1, W2, b2, out):
+    nc = tc.nc
+    with ExitStack() as stack:
+        keep = stack.enter_context(tc.tile_pool(name="keep", bufs=1))
+        work = stack.enter_context(tc.tile_pool(name="work", bufs=2))
+        operands = stack.enter_context(tc.tile_pool(name="operands", bufs=2))
+        hidden = stack.enter_context(tc.tile_pool(name="hidden", bufs=3))
+        acc_banks = stack.enter_context(tc.psum_pool(name="acc_banks", bufs=6))
+        out_banks = stack.enter_context(tc.psum_pool(name="out_banks", bufs=2))
+
+        p_rows = keep.tile([P, BATCHES, D], BF16)
+        v_rows = keep.tile([P, BATCHES, D], BF16)
+        nc.sync.dma_start(out=p_rows[:], in_=p.rearrange("b t n d -> (b t n) d").rearrange("(j r) d -> r j d", r=P))
+        nc.sync.dma_start(out=v_rows[:], in_=v.rearrange("b t m d -> (b t m) d").rearrange("(j r) d -> r j d", r=P))
+        w1_rows = keep.tile([P, PACK, F], BF16)
+        nc.sync.dma_start(out=w1_rows[:], in_=W1.rearrange("(q t) f -> q t f", t=PACK))
+        b1_bf16 = keep.tile([P, F_TILES], BF16)
+        nc.sync.dma_start(out=b1_bf16[:], in_=b1.rearrange("(i c) -> i c", c=F_TILES))
+        w2_rows = keep.tile([P, PACK, D], BF16)
+        nc.sync.dma_start(out=w2_rows[:], in_=W2.rearrange("(q t) d -> q t d", t=PACK))
+        b2_bf16 = keep.tile([P, D], BF16)
+        nc.sync.dma_start(out=b2_bf16[:], in_=b2.partition_broadcast(P))
+
+        p_packed = keep.tile([P, BATCHES * N * REPEAT + BATCHES * N], I32, align_bytes=64)
+        v_packed = keep.tile([P, BATCHES * M + BATCHES * M // 4], I32, align_bytes=64)
+        nc.vector.memset(p_packed[:, BATCHES * N * REPEAT :], 0)
+        nc.vector.memset(v_packed[:, BATCHES * M :], 0)
+        lane_tiles = []
+        for parity in range(2):
+            lane_tiles.append(
+                [keep.tile([P, PACKED], I32, name="lane_%d_%d" % (parity, g), align_bytes=64) for g in range(GROUPS)]
+            )
+            for g in (2, 3):
+                nc.vector.memset(lane_tiles[parity][g][:, PAIRS:], 0)
+
+        p_lanes = keep.tile([P, BATCHES, N, REPEAT, PACK], BF16, align_bytes=64)
+        v_lanes = keep.tile([P, BATCHES, M, PACK], BF16, align_bytes=64)
+        p_sorted = keep.tile([P, BATCHES, PACK, QUAD], BF16, align_bytes=64)
+        v_sorted = keep.tile([P, BATCHES, PACK, QUAD], BF16, align_bytes=64)
+        p_turned = keep.tile([P, BATCHES, PACK, N], BF16, align_bytes=64)
+        v_turned = keep.tile([P, BATCHES, PACK, M], BF16, align_bytes=64)
+        nc.vector.tensor_copy(out=p_sorted[:], in_=p_rows[:].rearrange("r j (q t) -> r j t q", t=PACK))
+        nc.vector.tensor_copy(out=v_sorted[:], in_=v_rows[:].rearrange("r j (q t) -> r j t q", t=PACK))
+        nc.vector.transpose(
+            out=p_turned[:].rearrange("r j t n -> r (j t n)"), in_=p_sorted[:].rearrange("r j t q -> r (j t q)")
+        )
+        nc.vector.transpose(
+            out=v_turned[:].rearrange("r j t m -> r (j t m)"), in_=v_sorted[:].rearrange("r j t q -> r (j t q)")
+        )
+        for j in range(BATCHES):
+            nc.vector.tensor_copy(
+                out=p_lanes[:, j],
+                in_=p_turned[:, j].rearrange("r t n -> r n t").unsqueeze(2).to_broadcast([P, N, REPEAT, PACK]),
+            )
+        nc.vector.tensor_copy(out=v_lanes[:], in_=v_turned[:].rearrange("r j t m -> r j m t"))
+        nc.vector.quantize_mx(
+            out=words_of(p_packed, 0, BATCHES * N * REPEAT),
+            scales=scales_of(p_packed, BATCHES * N * REPEAT, 0, BATCHES * N * REPEAT),
+            in_=p_lanes[:].rearrange("r j n e t -> r (j n e t)"),
+        )
+        nc.vector.quantize_mx(
+            out=words_of(v_packed, 0, BATCHES * M),
+            scales=scales_of(v_packed, BATCHES * M, 0, BATCHES * M),
+            in_=v_lanes[:].rearrange("r j m t -> r (j m t)"),
+        )
+
+        w1_grouped = keep.tile([P, F_TILES, P, PACK], BF16, align_bytes=64)
+        nc.scalar.copy(out=w1_grouped[:], in_=w1_rows[:].rearrange("q t (i c) -> q c i t", c=F_TILES))
+        w1_words = keep.tile([P, F], I32, align_bytes=64)
+        w1_scales = keep.tile([P, F], U8, align_bytes=64)
+        nc.vector.quantize_mx(
+            out=w1_words[:].bitcast(FP8X4), scales=w1_scales[:], in_=w1_grouped[:].rearrange("q c i t -> q (c i t)")
+        )
+        w2_grouped = keep.tile([P, D, PACK], BF16, align_bytes=64)
+        nc.scalar.copy(out=w2_grouped[:], in_=w2_rows[:].rearrange("q t d -> q d t"))
+        w2_words = keep.tile([P, D], I32, align_bytes=64)
+        w2_scales = keep.tile([P, D], U8, align_bytes=64)
+        nc.vector.quantize_mx(
+            out=w2_words[:].bitcast(FP8X4), scales=w2_scales[:], in_=w2_grouped[:].rearrange("q d t -> q (d t)")
+        )
+        b1_cols = keep.tile([P, F_TILES], F32)
+        nc.vector.tensor_copy(out=b1_cols[:], in_=b1_bf16[:])
+        b2_rows = keep.tile([P, D], F32)
+        nc.vector.tensor_copy(out=b2_rows[:], in_=b2_bf16[:])
+
+        def build_batch(j):
+            lanes = lane_tiles[j % 2]
+            p_all = p_lanes[:, j, :, 0, :].unsqueeze(2).to_broadcast([P, N, M, PACK])
+            v_all = v_lanes[:, j].unsqueeze(1).to_broadcast([P, N, M, PACK])
+
+            product = work.tile([P, N, M, PACK], BF16, align_bytes=64)
+            nc.vector.tensor_tensor(out=product[:], in0=p_all, in1=v_all, op=ALU.mult)
+            difference = work.tile([P, N, M, PACK], BF16, align_bytes=64)
+            nc.vector.tensor_tensor(out=difference[:], in0=p_all, in1=v_all, op=ALU.subtract)
+            distance = work.tile([P, N, M, PACK], BF16, align_bytes=64)
+            nc.scalar.activation(out=distance[:], in_=difference[:], func=ACT.Abs)
+            for g, values in ((2, product), (3, distance)):
+                nc.vector.quantize_mx(
+                    out=words_of(lanes[g], 0, PAIRS),
+                    scales=scales_of(lanes[g], PAIRS, 0, PAIRS),
+                    in_=values[:].rearrange("r n m t -> r (n m t)"),
+                )
+
+            p_words = p_packed[:, j * N * REPEAT : (j + 1) * N * REPEAT].rearrange("r (n e) -> r n e", e=REPEAT)
+            p_plane = p_packed[:, BATCHES * N * REPEAT + j * N : BATCHES * N * REPEAT + (j + 1) * N]
+            nc.vector.tensor_copy(
+                out=lanes[0][:, :PAIRS].rearrange("r (n s e) -> r n s e", s=M // REPEAT, e=REPEAT),
+                in_=p_words.unsqueeze(2).to_broadcast([P, N, M // REPEAT, REPEAT]),
+            )
+            nc.vector.tensor_copy(
+                out=lanes[0][:, PAIRS:].rearrange("r (n s) -> r n s", s=M // 4),
+                in_=p_plane.unsqueeze(2).to_broadcast([P, N, M // 4]),
+            )
+            v_words = v_packed[:, j * M : (j + 1) * M]
+            v_plane = v_packed[:, BATCHES * M + j * M // 4 : BATCHES * M + (j + 1) * M // 4]
+            nc.vector.tensor_copy(
+                out=lanes[1][:, :PAIRS].rearrange("r (n m) -> r n m", m=M),
+                in_=v_words.unsqueeze(1).to_broadcast([P, N, M]),
+            )
+            nc.vector.tensor_copy(
+                out=lanes[1][:, PAIRS:].rearrange("r (n s) -> r n s", s=M // 4),
+                in_=v_plane.unsqueeze(1).to_broadcast([P, N, M // 4]),
+            )
+
+            pair_mx = operands.tile([P, LANES, PACKED], I32, align_bytes=64)
+            for g in range(GROUPS):
+                for a in range(LANES):
+                    nc.sync.dma_start(
+                        out=pair_mx[g * QUAD : (g + 1) * QUAD, a, :], in_=lanes[g][a * QUAD : (a + 1) * QUAD, :]
+                    )
+            return pair_mx
+
+        out_tiles = out.rearrange("b t (h s r) d -> (b t) h r s d", h=CHUNKS, s=ROW_TILES, r=P)
+
+        def run_chunk(pair_mx, grid, a, half):
+            packed = pair_mx[:, a, :]
+            planes = hidden.tile([P, F_TILES, CHUNK], BF16)
+            for c in range(F_TILES):
+                acc = acc_banks.tile([P, CHUNK], F32)
+                nc.tensor.matmul_mx(
+                    out=acc[:],
+                    lhsT=w1_words[:, c * P : (c + 1) * P].bitcast(FP8X4),
+                    lhsT_scale=w1_scales[:, c * P : (c + 1) * P],
+                    rhs=words_of(packed, half * CHUNK, CHUNK),
+                    rhs_scale=scales_of(packed, PAIRS, half * CHUNK, CHUNK),
+                    start=True,
+                    stop=True,
+                )
+                nc.scalar.activation(out=planes[:, c, :], in_=acc[:], func=ACT.Silu, bias=b1_cols[:, c : c + 1])
+            grouped = hidden.tile([P, CHUNK, PACK], BF16, align_bytes=64)
+            nc.vector.tensor_copy(
+                out=grouped[:].rearrange("i (w e) c -> i w c e", e=4),
+                in_=planes[:].rearrange("i c (w e) -> i w c e", e=4),
+            )
+            h_words = hidden.tile([P, CHUNK], I32, align_bytes=64)
+            h_scales = hidden.tile([P, CHUNK], U8, align_bytes=64)
+            nc.vector.quantize_mx(
+                out=h_words[:].bitcast(FP8X4), scales=h_scales[:], in_=grouped[:].rearrange("i w c -> i (w c)")
+            )
+            grid_acc = out_banks.tile([P, ROW_TILES, D], F32)
+            for s in range(ROW_TILES):
+                nc.tensor.matmul_mx(
+                    out=grid_acc[:, s, :],
+                    lhsT=h_words[:, s * P : (s + 1) * P].bitcast(FP8X4),
+                    lhsT_scale=h_scales[:, s * P : (s + 1) * P],
+                    rhs=w2_words[:].bitcast(FP8X4),
+                    rhs_scale=w2_scales[:],
+                    start=True,
+                    stop=True,
+                )
+            result = hidden.tile([P, ROW_TILES, D], F32)
+            nc.vector.tensor_tensor(
+                out=result[:], in0=grid_acc[:], in1=b2_rows[:].unsqueeze(1).to_broadcast([P, ROW_TILES, D]), op=ALU.add
+            )
+            nc.gpsimd.dma_start(out=out_tiles[grid, half], in_=result[:])
+
+        pair_next = build_batch(0)
+        for j in range(BATCHES):
+            pair_now = pair_next
+            if j + 1 < BATCHES:
+                pair_next = build_batch(j + 1)
+            for a in range(LANES):
+                for half in range(CHUNKS):
+                    run_chunk(pair_now, LANES * j + a, a, half)

@@ -26,6 +26,7 @@ CHUNK = 512
 CHUNKS = PAIRS // CHUNK
 F_TILES = F // P
 ROW_TILES = CHUNK // P
+AHEAD = 2
 REPEAT = 4
 
 PLANE = PAIRS // 4
@@ -45,9 +46,10 @@ def scales_of(packed, words, first, count):
 def tile_pairinteractiongrid_pa_t_kernel(tc, p, v, W1, b1, W2, b2, out):
     nc = tc.nc
     with ExitStack() as stack:
+        stack.enter_context(tc.manual_schedule())
         keep = stack.enter_context(tc.tile_pool(name="keep", bufs=1))
         work = stack.enter_context(tc.tile_pool(name="work", bufs=2))
-        operands = stack.enter_context(tc.tile_pool(name="operands", bufs=2))
+        operands = stack.enter_context(tc.tile_pool(name="operands", bufs=AHEAD + 1))
         hidden = stack.enter_context(tc.tile_pool(name="hidden", bufs=3))
         acc_banks = stack.enter_context(tc.psum_pool(name="acc_banks", bufs=6))
         out_banks = stack.enter_context(tc.psum_pool(name="out_banks", bufs=2))
@@ -58,12 +60,12 @@ def tile_pairinteractiongrid_pa_t_kernel(tc, p, v, W1, b1, W2, b2, out):
         nc.sync.dma_start(out=v_rows[:], in_=v.rearrange("b t m d -> (b t m) d").rearrange("(j r) d -> r j d", r=P))
         w1_rows = keep.tile([P, PACK, F], BF16)
         nc.sync.dma_start(out=w1_rows[:], in_=W1.rearrange("(q t) f -> q t f", t=PACK))
-        b1_bf16 = keep.tile([P, F_TILES], BF16)
-        nc.sync.dma_start(out=b1_bf16[:], in_=b1.rearrange("(i c) -> i c", c=F_TILES))
         w2_rows = keep.tile([P, PACK, D], BF16)
         nc.sync.dma_start(out=w2_rows[:], in_=W2.rearrange("(q t) d -> q t d", t=PACK))
-        b2_bf16 = keep.tile([P, D], BF16)
-        nc.sync.dma_start(out=b2_bf16[:], in_=b2.partition_broadcast(P))
+        b1_cols = keep.tile([P, F_TILES], BF16)
+        nc.sync.dma_start(out=b1_cols[:], in_=b1.rearrange("(i c) -> i c", c=F_TILES))
+        b2_rows = keep.tile([P, D], BF16)
+        nc.sync.dma_start(out=b2_rows[:], in_=b2.partition_broadcast(P))
 
         p_packed = keep.tile([P, BATCHES * N * REPEAT + BATCHES * N], I32, align_bytes=64)
         v_packed = keep.tile([P, BATCHES * M + BATCHES * M // 4], I32, align_bytes=64)
@@ -76,6 +78,15 @@ def tile_pairinteractiongrid_pa_t_kernel(tc, p, v, W1, b1, W2, b2, out):
             )
             for g in (2, 3):
                 nc.vector.memset(lane_tiles[parity][g][:, PAIRS:], 0)
+
+        w1_grouped = keep.tile([P, F_TILES, P, PACK], BF16, align_bytes=64)
+        nc.scalar.copy(out=w1_grouped[:], in_=w1_rows[:].rearrange("q t (i c) -> q c i t", c=F_TILES))
+        w2_grouped = keep.tile([P, D, PACK], BF16, align_bytes=64)
+        nc.scalar.copy(out=w2_grouped[:], in_=w2_rows[:].rearrange("q t d -> q d t"))
+        w1_words = keep.tile([P, F], I32, align_bytes=64)
+        w1_scales = keep.tile([P, F], U8, align_bytes=64)
+        w2_words = keep.tile([P, D], I32, align_bytes=64)
+        w2_scales = keep.tile([P, D], U8, align_bytes=64)
 
         p_lanes = keep.tile([P, BATCHES, N, REPEAT, PACK], BF16, align_bytes=64)
         v_lanes = keep.tile([P, BATCHES, M, PACK], BF16, align_bytes=64)
@@ -97,110 +108,131 @@ def tile_pairinteractiongrid_pa_t_kernel(tc, p, v, W1, b1, W2, b2, out):
                 in_=p_turned[:, j].rearrange("r t n -> r n t").unsqueeze(2).to_broadcast([P, N, REPEAT, PACK]),
             )
         nc.vector.tensor_copy(out=v_lanes[:], in_=v_turned[:].rearrange("r j t m -> r j m t"))
-        nc.vector.quantize_mx(
-            out=words_of(p_packed, 0, BATCHES * N * REPEAT),
-            scales=scales_of(p_packed, BATCHES * N * REPEAT, 0, BATCHES * N * REPEAT),
-            in_=p_lanes[:].rearrange("r j n e t -> r (j n e t)"),
-        )
-        nc.vector.quantize_mx(
-            out=words_of(v_packed, 0, BATCHES * M),
-            scales=scales_of(v_packed, BATCHES * M, 0, BATCHES * M),
-            in_=v_lanes[:].rearrange("r j m t -> r (j m t)"),
-        )
 
-        w1_grouped = keep.tile([P, F_TILES, P, PACK], BF16, align_bytes=64)
-        nc.scalar.copy(out=w1_grouped[:], in_=w1_rows[:].rearrange("q t (i c) -> q c i t", c=F_TILES))
-        w1_words = keep.tile([P, F], I32, align_bytes=64)
-        w1_scales = keep.tile([P, F], U8, align_bytes=64)
-        nc.vector.quantize_mx(
-            out=w1_words[:].bitcast(FP8X4), scales=w1_scales[:], in_=w1_grouped[:].rearrange("q c i t -> q (c i t)")
-        )
-        w2_grouped = keep.tile([P, D, PACK], BF16, align_bytes=64)
-        nc.scalar.copy(out=w2_grouped[:], in_=w2_rows[:].rearrange("q t d -> q d t"))
-        w2_words = keep.tile([P, D], I32, align_bytes=64)
-        w2_scales = keep.tile([P, D], U8, align_bytes=64)
-        nc.vector.quantize_mx(
-            out=w2_words[:].bitcast(FP8X4), scales=w2_scales[:], in_=w2_grouped[:].rearrange("q d t -> q (d t)")
-        )
-        b1_cols = keep.tile([P, F_TILES], F32)
-        nc.vector.tensor_copy(out=b1_cols[:], in_=b1_bf16[:])
-        b2_rows = keep.tile([P, D], F32)
-        nc.vector.tensor_copy(out=b2_rows[:], in_=b2_bf16[:])
+        def quantise_inputs():
+            nc.vector.quantize_mx(
+                out=words_of(p_packed, 0, BATCHES * N * REPEAT),
+                scales=scales_of(p_packed, BATCHES * N * REPEAT, 0, BATCHES * N * REPEAT),
+                in_=p_lanes[:].rearrange("r j n e t -> r (j n e t)"),
+            )
+            nc.vector.quantize_mx(
+                out=words_of(v_packed, 0, BATCHES * M),
+                scales=scales_of(v_packed, BATCHES * M, 0, BATCHES * M),
+                in_=v_lanes[:].rearrange("r j m t -> r (j m t)"),
+            )
+            nc.vector.quantize_mx(
+                out=w1_words[:].bitcast(FP8X4),
+                scales=w1_scales[:],
+                in_=w1_grouped[:].rearrange("q c i t -> q (c i t)"),
+            )
+            nc.vector.quantize_mx(
+                out=w2_words[:].bitcast(FP8X4), scales=w2_scales[:], in_=w2_grouped[:].rearrange("q d t -> q (d t)")
+            )
 
-        def build_batch(j):
+        def batch_steps(j):
             lanes = lane_tiles[j % 2]
+            pair_mx = operands.tile([P, LANES, PACKED], I32, align_bytes=64)
             p_all = p_lanes[:, j, :, 0, :].unsqueeze(2).to_broadcast([P, N, M, PACK])
             v_all = v_lanes[:, j].unsqueeze(1).to_broadcast([P, N, M, PACK])
-
             product = work.tile([P, N, M, PACK], BF16, align_bytes=64)
-            nc.vector.tensor_tensor(out=product[:], in0=p_all, in1=v_all, op=ALU.mult)
-            difference = work.tile([P, N, M, PACK], BF16, align_bytes=64)
-            nc.vector.tensor_tensor(out=difference[:], in0=p_all, in1=v_all, op=ALU.subtract)
             distance = work.tile([P, N, M, PACK], BF16, align_bytes=64)
-            nc.scalar.activation(out=distance[:], in_=difference[:], func=ACT.Abs)
-            for g, values in ((2, product), (3, distance)):
+
+            def to_operand_layout(g):
+                for a in range(LANES):
+                    nc.sync.dma_start(
+                        out=pair_mx[g * QUAD : (g + 1) * QUAD, a, :], in_=lanes[g][a * QUAD : (a + 1) * QUAD, :]
+                    )
+
+            def quantise(g, values):
                 nc.vector.quantize_mx(
                     out=words_of(lanes[g], 0, PAIRS),
                     scales=scales_of(lanes[g], PAIRS, 0, PAIRS),
                     in_=values[:].rearrange("r n m t -> r (n m t)"),
                 )
+                to_operand_layout(g)
 
-            p_words = p_packed[:, j * N * REPEAT : (j + 1) * N * REPEAT].rearrange("r (n e) -> r n e", e=REPEAT)
-            p_plane = p_packed[:, BATCHES * N * REPEAT + j * N : BATCHES * N * REPEAT + (j + 1) * N]
-            nc.vector.tensor_copy(
-                out=lanes[0][:, :PAIRS].rearrange("r (n s e) -> r n s e", s=M // REPEAT, e=REPEAT),
-                in_=p_words.unsqueeze(2).to_broadcast([P, N, M // REPEAT, REPEAT]),
-            )
-            nc.vector.tensor_copy(
-                out=lanes[0][:, PAIRS:].rearrange("r (n s) -> r n s", s=M // 4),
-                in_=p_plane.unsqueeze(2).to_broadcast([P, N, M // 4]),
-            )
-            v_words = v_packed[:, j * M : (j + 1) * M]
-            v_plane = v_packed[:, BATCHES * M + j * M // 4 : BATCHES * M + (j + 1) * M // 4]
-            nc.vector.tensor_copy(
-                out=lanes[1][:, :PAIRS].rearrange("r (n m) -> r n m", m=M),
-                in_=v_words.unsqueeze(1).to_broadcast([P, N, M]),
-            )
-            nc.vector.tensor_copy(
-                out=lanes[1][:, PAIRS:].rearrange("r (n s) -> r n s", s=M // 4),
-                in_=v_plane.unsqueeze(1).to_broadcast([P, N, M // 4]),
-            )
+            def subtract():
+                nc.vector.tensor_tensor(out=distance[:], in0=p_all, in1=v_all, op=ALU.subtract)
 
-            pair_mx = operands.tile([P, LANES, PACKED], I32, align_bytes=64)
-            for g in range(GROUPS):
-                for a in range(LANES):
-                    nc.sync.dma_start(
-                        out=pair_mx[g * QUAD : (g + 1) * QUAD, a, :], in_=lanes[g][a * QUAD : (a + 1) * QUAD, :]
-                    )
-            return pair_mx
+            def multiply():
+                nc.scalar.activation(out=distance[:], in_=distance[:], func=ACT.Abs)
+                nc.vector.tensor_tensor(out=product[:], in0=p_all, in1=v_all, op=ALU.mult)
 
-        out_tiles = out.rearrange("b t (h s r) d -> (b t) h r s d", h=CHUNKS, s=ROW_TILES, r=P)
+            def repeat_p():
+                first = BATCHES * N * REPEAT
+                nc.vector.tensor_copy(
+                    out=lanes[0][:, :PAIRS].rearrange("r (n s e) -> r n s e", s=M // REPEAT, e=REPEAT),
+                    in_=p_packed[:, j * N * REPEAT : (j + 1) * N * REPEAT]
+                    .rearrange("r (n e) -> r n e", e=REPEAT)
+                    .unsqueeze(2)
+                    .to_broadcast([P, N, M // REPEAT, REPEAT]),
+                )
+                nc.vector.tensor_copy(
+                    out=lanes[0][:, PAIRS:].rearrange("r (n s) -> r n s", s=M // 4),
+                    in_=p_packed[:, first + j * N : first + (j + 1) * N].unsqueeze(2).to_broadcast([P, N, M // 4]),
+                )
+                to_operand_layout(0)
 
-        def run_chunk(pair_mx, grid, a, half):
-            packed = pair_mx[:, a, :]
-            planes = hidden.tile([P, F_TILES, CHUNK], BF16)
+            def repeat_v():
+                first = BATCHES * M
+                nc.vector.tensor_copy(
+                    out=lanes[1][:, :PAIRS].rearrange("r (n m) -> r n m", m=M),
+                    in_=v_packed[:, j * M : (j + 1) * M].unsqueeze(1).to_broadcast([P, N, M]),
+                )
+                nc.vector.tensor_copy(
+                    out=lanes[1][:, PAIRS:].rearrange("r (n s) -> r n s", s=M // 4),
+                    in_=v_packed[:, first + j * M // 4 : first + (j + 1) * M // 4]
+                    .unsqueeze(1)
+                    .to_broadcast([P, N, M // 4]),
+                )
+                to_operand_layout(1)
+
+            steps = [subtract, multiply, repeat_p, repeat_v, lambda: quantise(2, product), lambda: quantise(3, distance)]
+            return pair_mx, steps
+
+        out_tiles = out.rearrange("b t (h s r) d -> (b t h) r s d", h=CHUNKS, s=ROW_TILES, r=P)
+        pair_tiles = {}
+        planes_of = {}
+        grouped_of = {}
+        hidden_mx_of = {}
+        grid_acc_of = {}
+
+        def first_layer(k):
+            packed = pair_tiles[k // (LANES * CHUNKS)][:, (k // CHUNKS) % LANES, :]
+            first = (k % CHUNKS) * CHUNK
+            planes = hidden.tile([P, F_TILES, CHUNK], BF16, bufs=4)
             for c in range(F_TILES):
                 acc = acc_banks.tile([P, CHUNK], F32)
                 nc.tensor.matmul_mx(
                     out=acc[:],
                     lhsT=w1_words[:, c * P : (c + 1) * P].bitcast(FP8X4),
                     lhsT_scale=w1_scales[:, c * P : (c + 1) * P],
-                    rhs=words_of(packed, half * CHUNK, CHUNK),
-                    rhs_scale=scales_of(packed, PAIRS, half * CHUNK, CHUNK),
+                    rhs=words_of(packed, first, CHUNK),
+                    rhs_scale=scales_of(packed, PAIRS, first, CHUNK),
                     start=True,
                     stop=True,
                 )
                 nc.scalar.activation(out=planes[:, c, :], in_=acc[:], func=ACT.Silu, bias=b1_cols[:, c : c + 1])
+            planes_of[k] = planes
+
+        def regroup(k):
             grouped = hidden.tile([P, CHUNK, PACK], BF16, align_bytes=64)
             nc.vector.tensor_copy(
                 out=grouped[:].rearrange("i (w e) c -> i w c e", e=4),
-                in_=planes[:].rearrange("i c (w e) -> i w c e", e=4),
+                in_=planes_of[k][:].rearrange("i c (w e) -> i w c e", e=4),
             )
+            grouped_of[k] = grouped
+
+        def quantise_hidden(k):
             h_words = hidden.tile([P, CHUNK], I32, align_bytes=64)
             h_scales = hidden.tile([P, CHUNK], U8, align_bytes=64)
             nc.vector.quantize_mx(
-                out=h_words[:].bitcast(FP8X4), scales=h_scales[:], in_=grouped[:].rearrange("i w c -> i (w c)")
+                out=h_words[:].bitcast(FP8X4), scales=h_scales[:], in_=grouped_of[k][:].rearrange("i w c -> i (w c)")
             )
+            hidden_mx_of[k] = (h_words, h_scales)
+
+        def second_layer(k):
+            h_words, h_scales = hidden_mx_of[k]
             grid_acc = out_banks.tile([P, ROW_TILES, D], F32)
             for s in range(ROW_TILES):
                 nc.tensor.matmul_mx(
@@ -212,17 +244,41 @@ def tile_pairinteractiongrid_pa_t_kernel(tc, p, v, W1, b1, W2, b2, out):
                     start=True,
                     stop=True,
                 )
+            grid_acc_of[k] = grid_acc
+
+        def finish(k):
             result = hidden.tile([P, ROW_TILES, D], F32)
             nc.vector.tensor_tensor(
-                out=result[:], in0=grid_acc[:], in1=b2_rows[:].unsqueeze(1).to_broadcast([P, ROW_TILES, D]), op=ALU.add
+                out=result[:],
+                in0=grid_acc_of[k][:],
+                in1=b2_rows[:].unsqueeze(1).to_broadcast([P, ROW_TILES, D]),
+                op=ALU.add,
             )
-            nc.gpsimd.dma_start(out=out_tiles[grid, half], in_=result[:])
+            nc.sync.dma_start(out=out_tiles[k], in_=result[:])
 
-        pair_next = build_batch(0)
-        for j in range(BATCHES):
-            pair_now = pair_next
-            if j + 1 < BATCHES:
-                pair_next = build_batch(j + 1)
-            for a in range(LANES):
-                for half in range(CHUNKS):
-                    run_chunk(pair_now, LANES * j + a, a, half)
+        quantise_inputs()
+        for j in range(AHEAD):
+            pair_tiles[j], steps = batch_steps(j)
+            for step in steps:
+                step()
+
+        rounds_per_batch = LANES * CHUNKS
+        total = BATCHES * rounds_per_batch
+        steps = []
+        for k in range(total + 3):
+            if 0 <= k - 3 < total:
+                second_layer(k - 3)
+            if k < total:
+                first_layer(k)
+            if 0 <= k - 1 < total:
+                regroup(k - 1)
+            if 0 <= k - 2 < total:
+                quantise_hidden(k - 2)
+            if 0 <= k - 3 < total:
+                finish(k - 3)
+            j = k // rounds_per_batch + AHEAD
+            number = k % rounds_per_batch
+            if number == 0 and j < BATCHES:
+                pair_tiles[j], steps = batch_steps(j)
+            if j < BATCHES and number < len(steps):
+                steps[number]()

@@ -1,6 +1,7 @@
 from contextlib import ExitStack
 
 import concourse.mybir as mybir
+from concourse.masks import make_identity
 
 BF16 = mybir.dt.bfloat16
 F32 = mybir.dt.float32
@@ -23,11 +24,12 @@ LANES = 4
 BATCHES = GRIDS // LANES
 PAIRS = N * M
 CHUNK = 512
-CHUNKS = PAIRS // CHUNK
+ROUNDS = LANES * PAIRS // CHUNK
 F_TILES = F // P
 ROW_TILES = CHUNK // P
 AHEAD = 2
 REPEAT = 4
+SLICE = N // ROUNDS
 
 PLANE = PAIRS // 4
 PACKED = PAIRS + PLANE
@@ -58,6 +60,10 @@ def tile_pairinteractiongrid_pa_t_kernel(tc, p, v, W1, b1, W2, b2, out):
         v_rows = keep.tile([P, BATCHES, D], BF16)
         nc.sync.dma_start(out=p_rows[:], in_=p.rearrange("b t n d -> (b t n) d").rearrange("(j r) d -> r j d", r=P))
         nc.sync.dma_start(out=v_rows[:], in_=v.rearrange("b t m d -> (b t m) d").rearrange("(j r) d -> r j d", r=P))
+        points = keep.tile([P, GRIDS, D], BF16)
+        nc.sync.dma_start(out=points[0:N], in_=p.rearrange("b t n d -> n (b t) d"))
+        nc.sync.dma_start(out=points[N : N + M], in_=v.rearrange("b t m d -> m (b t) d"))
+        nc.vector.memset(points[N + M :], 0.0)
         w1_rows = keep.tile([P, PACK, F], BF16)
         nc.sync.dma_start(out=w1_rows[:], in_=W1.rearrange("(q t) f -> q t f", t=PACK))
         w2_rows = keep.tile([P, PACK, D], BF16)
@@ -79,14 +85,15 @@ def tile_pairinteractiongrid_pa_t_kernel(tc, p, v, W1, b1, W2, b2, out):
             for g in (2, 3):
                 nc.vector.memset(lane_tiles[parity][g][:, PAIRS:], 0)
 
-        w1_grouped = keep.tile([P, F_TILES, P, PACK], BF16, align_bytes=64)
-        nc.scalar.copy(out=w1_grouped[:], in_=w1_rows[:].rearrange("q t (i c) -> q c i t", c=F_TILES))
-        w2_grouped = keep.tile([P, D, PACK], BF16, align_bytes=64)
-        nc.scalar.copy(out=w2_grouped[:], in_=w2_rows[:].rearrange("q t d -> q d t"))
-        w1_words = keep.tile([P, F], I32, align_bytes=64)
-        w1_scales = keep.tile([P, F], U8, align_bytes=64)
-        w2_words = keep.tile([P, D], I32, align_bytes=64)
-        w2_scales = keep.tile([P, D], U8, align_bytes=64)
+        identity = keep.tile([P, P], BF16)
+        make_identity(nc, identity[:])
+        selector = keep.tile([P, N, M], BF16)
+        nc.vector.tensor_tensor(
+            out=selector[:],
+            in0=identity[:, 0:N].unsqueeze(2).to_broadcast([P, N, M]),
+            in1=identity[:, N : N + M].unsqueeze(1).to_broadcast([P, N, M]),
+            op=ALU.subtract,
+        )
 
         p_lanes = keep.tile([P, BATCHES, N, REPEAT, PACK], BF16, align_bytes=64)
         v_lanes = keep.tile([P, BATCHES, M, PACK], BF16, align_bytes=64)
@@ -95,7 +102,7 @@ def tile_pairinteractiongrid_pa_t_kernel(tc, p, v, W1, b1, W2, b2, out):
         p_turned = keep.tile([P, BATCHES, PACK, N], BF16, align_bytes=64)
         v_turned = keep.tile([P, BATCHES, PACK, M], BF16, align_bytes=64)
         nc.vector.tensor_copy(out=p_sorted[:], in_=p_rows[:].rearrange("r j (q t) -> r j t q", t=PACK))
-        nc.vector.tensor_copy(out=v_sorted[:], in_=v_rows[:].rearrange("r j (q t) -> r j t q", t=PACK))
+        nc.scalar.copy(out=v_sorted[:], in_=v_rows[:].rearrange("r j (q t) -> r j t q", t=PACK))
         nc.vector.transpose(
             out=p_turned[:].rearrange("r j t n -> r (j t n)"), in_=p_sorted[:].rearrange("r j t q -> r (j t q)")
         )
@@ -107,102 +114,118 @@ def tile_pairinteractiongrid_pa_t_kernel(tc, p, v, W1, b1, W2, b2, out):
                 out=p_lanes[:, j],
                 in_=p_turned[:, j].rearrange("r t n -> r n t").unsqueeze(2).to_broadcast([P, N, REPEAT, PACK]),
             )
-        nc.vector.tensor_copy(out=v_lanes[:], in_=v_turned[:].rearrange("r j t m -> r j m t"))
+        nc.scalar.copy(out=v_lanes[:], in_=v_turned[:].rearrange("r j t m -> r j m t"))
+        nc.vector.quantize_mx(
+            out=words_of(p_packed, 0, BATCHES * N * REPEAT),
+            scales=scales_of(p_packed, BATCHES * N * REPEAT, 0, BATCHES * N * REPEAT),
+            in_=p_lanes[:].rearrange("r j n e t -> r (j n e t)"),
+        )
+        nc.vector.quantize_mx(
+            out=words_of(v_packed, 0, BATCHES * M),
+            scales=scales_of(v_packed, BATCHES * M, 0, BATCHES * M),
+            in_=v_lanes[:].rearrange("r j m t -> r (j m t)"),
+        )
 
-        def quantise_inputs():
-            nc.vector.quantize_mx(
-                out=words_of(p_packed, 0, BATCHES * N * REPEAT),
-                scales=scales_of(p_packed, BATCHES * N * REPEAT, 0, BATCHES * N * REPEAT),
-                in_=p_lanes[:].rearrange("r j n e t -> r (j n e t)"),
-            )
-            nc.vector.quantize_mx(
-                out=words_of(v_packed, 0, BATCHES * M),
-                scales=scales_of(v_packed, BATCHES * M, 0, BATCHES * M),
-                in_=v_lanes[:].rearrange("r j m t -> r (j m t)"),
-            )
-            nc.vector.quantize_mx(
-                out=w1_words[:].bitcast(FP8X4),
-                scales=w1_scales[:],
-                in_=w1_grouped[:].rearrange("q c i t -> q (c i t)"),
-            )
-            nc.vector.quantize_mx(
-                out=w2_words[:].bitcast(FP8X4), scales=w2_scales[:], in_=w2_grouped[:].rearrange("q d t -> q (d t)")
-            )
-
-        def batch_steps(j):
-            lanes = lane_tiles[j % 2]
-            pair_mx = operands.tile([P, LANES, PACKED], I32, align_bytes=64)
-            p_all = p_lanes[:, j, :, 0, :].unsqueeze(2).to_broadcast([P, N, M, PACK])
-            v_all = v_lanes[:, j].unsqueeze(1).to_broadcast([P, N, M, PACK])
-            product = work.tile([P, N, M, PACK], BF16, align_bytes=64)
-            distance = work.tile([P, N, M, PACK], BF16, align_bytes=64)
-
-            def to_operand_layout(g):
-                for a in range(LANES):
-                    nc.sync.dma_start(
-                        out=pair_mx[g * QUAD : (g + 1) * QUAD, a, :], in_=lanes[g][a * QUAD : (a + 1) * QUAD, :]
-                    )
-
-            def quantise(g, values):
-                nc.vector.quantize_mx(
-                    out=words_of(lanes[g], 0, PAIRS),
-                    scales=scales_of(lanes[g], PAIRS, 0, PAIRS),
-                    in_=values[:].rearrange("r n m t -> r (n m t)"),
-                )
-                to_operand_layout(g)
-
-            def subtract():
-                nc.vector.tensor_tensor(out=distance[:], in0=p_all, in1=v_all, op=ALU.subtract)
-
-            def multiply():
-                nc.scalar.activation(out=distance[:], in_=distance[:], func=ACT.Abs)
-                nc.vector.tensor_tensor(out=product[:], in0=p_all, in1=v_all, op=ALU.mult)
-
-            def repeat_p():
-                first = BATCHES * N * REPEAT
-                nc.vector.tensor_copy(
-                    out=lanes[0][:, :PAIRS].rearrange("r (n s e) -> r n s e", s=M // REPEAT, e=REPEAT),
-                    in_=p_packed[:, j * N * REPEAT : (j + 1) * N * REPEAT]
-                    .rearrange("r (n e) -> r n e", e=REPEAT)
-                    .unsqueeze(2)
-                    .to_broadcast([P, N, M // REPEAT, REPEAT]),
-                )
-                nc.vector.tensor_copy(
-                    out=lanes[0][:, PAIRS:].rearrange("r (n s) -> r n s", s=M // 4),
-                    in_=p_packed[:, first + j * N : first + (j + 1) * N].unsqueeze(2).to_broadcast([P, N, M // 4]),
-                )
-                to_operand_layout(0)
-
-            def repeat_v():
-                first = BATCHES * M
-                nc.vector.tensor_copy(
-                    out=lanes[1][:, :PAIRS].rearrange("r (n m) -> r n m", m=M),
-                    in_=v_packed[:, j * M : (j + 1) * M].unsqueeze(1).to_broadcast([P, N, M]),
-                )
-                nc.vector.tensor_copy(
-                    out=lanes[1][:, PAIRS:].rearrange("r (n s) -> r n s", s=M // 4),
-                    in_=v_packed[:, first + j * M // 4 : first + (j + 1) * M // 4]
-                    .unsqueeze(1)
-                    .to_broadcast([P, N, M // 4]),
-                )
-                to_operand_layout(1)
-
-            steps = [subtract, multiply, repeat_p, repeat_v, lambda: quantise(2, product), lambda: quantise(3, distance)]
-            return pair_mx, steps
-
-        out_tiles = out.rearrange("b t (h s r) d -> (b t h) r s d", h=CHUNKS, s=ROW_TILES, r=P)
         pair_tiles = {}
+        distance_of = {}
+        product_of = {}
+
+        def open_batch(j):
+            pair_tiles[j] = operands.tile([P, LANES, PACKED], I32, name="pair_mx", align_bytes=64)
+            distance_of[j] = work.tile([P, N, M, PACK], BF16, name="distance", align_bytes=64)
+
+        def distances(j, w):
+            some = slice(w * SLICE, (w + 1) * SLICE)
+            by_feature = points[:, j * LANES : (j + 1) * LANES, :].rearrange("k a (q t) -> k t (a q)", t=PACK)
+            bank = acc_banks.tile([P, PACK, SLICE * M], F32, tag="acc")
+            for t in range(PACK):
+                nc.tensor.matmul(
+                    out=bank[:, t, :],
+                    lhsT=by_feature[:, t, :],
+                    rhs=selector[:, some, :].rearrange("k n m -> k (n m)"),
+                    start=True,
+                    stop=True,
+                )
+            nc.scalar.activation(
+                out=distance_of[j][:, some].rearrange("r n m t -> r (n m) t"),
+                in_=bank[:].rearrange("r t w -> r w t"),
+                func=ACT.Abs,
+            )
+
+        def to_operand_layout(j, g):
+            lanes = lane_tiles[j % 2][g]
+            for a in range(LANES):
+                nc.sync.dma_start(
+                    out=pair_tiles[j][g * QUAD : (g + 1) * QUAD, a, :], in_=lanes[a * QUAD : (a + 1) * QUAD, :]
+                )
+
+        def quantise_group(j, g, values):
+            lanes = lane_tiles[j % 2][g]
+            nc.vector.quantize_mx(
+                out=words_of(lanes, 0, PAIRS),
+                scales=scales_of(lanes, PAIRS, 0, PAIRS),
+                in_=values[:].rearrange("r n m t -> r (n m t)"),
+            )
+            to_operand_layout(j, g)
+
+        def multiply(j):
+            product_of[j] = work.tile([P, N, M, PACK], BF16, name="product", align_bytes=64)
+            nc.vector.tensor_tensor(
+                out=product_of[j][:],
+                in0=p_lanes[:, j, :, 0, :].unsqueeze(2).to_broadcast([P, N, M, PACK]),
+                in1=v_lanes[:, j].unsqueeze(1).to_broadcast([P, N, M, PACK]),
+                op=ALU.mult,
+            )
+
+        def repeat_p(j):
+            lanes = lane_tiles[j % 2][0]
+            first = BATCHES * N * REPEAT
+            nc.vector.tensor_copy(
+                out=lanes[:, :PAIRS].rearrange("r (n s e) -> r n s e", s=M // REPEAT, e=REPEAT),
+                in_=p_packed[:, j * N * REPEAT : (j + 1) * N * REPEAT]
+                .rearrange("r (n e) -> r n e", e=REPEAT)
+                .unsqueeze(2)
+                .to_broadcast([P, N, M // REPEAT, REPEAT]),
+            )
+            nc.vector.tensor_copy(
+                out=lanes[:, PAIRS:].rearrange("r (n s) -> r n s", s=M // 4),
+                in_=p_packed[:, first + j * N : first + (j + 1) * N].unsqueeze(2).to_broadcast([P, N, M // 4]),
+            )
+            to_operand_layout(j, 0)
+
+        def repeat_v(j):
+            lanes = lane_tiles[j % 2][1]
+            first = BATCHES * M
+            nc.vector.tensor_copy(
+                out=lanes[:, :PAIRS].rearrange("r (n m) -> r n m", m=M),
+                in_=v_packed[:, j * M : (j + 1) * M].unsqueeze(1).to_broadcast([P, N, M]),
+            )
+            nc.vector.tensor_copy(
+                out=lanes[:, PAIRS:].rearrange("r (n s) -> r n s", s=M // 4),
+                in_=v_packed[:, first + j * M // 4 : first + (j + 1) * M // 4].unsqueeze(1).to_broadcast([P, N, M // 4]),
+            )
+            to_operand_layout(j, 1)
+
+        def vector_steps(j):
+            return [
+                lambda: multiply(j),
+                lambda: repeat_p(j),
+                lambda: repeat_v(j),
+                lambda: quantise_group(j, 2, product_of[j]),
+            ]
+
+        out_tiles = out.rearrange("b t (h s r) d -> (b t h) r s d", s=ROW_TILES, r=P)
         planes_of = {}
         grouped_of = {}
         hidden_mx_of = {}
         grid_acc_of = {}
 
         def first_layer(k):
-            packed = pair_tiles[k // (LANES * CHUNKS)][:, (k // CHUNKS) % LANES, :]
-            first = (k % CHUNKS) * CHUNK
+            packed = pair_tiles[k // ROUNDS][:, (k % ROUNDS) * CHUNK // PAIRS, :]
+            first = k * CHUNK % PAIRS
             planes = hidden.tile([P, F_TILES, CHUNK], BF16, bufs=4)
             for c in range(F_TILES):
-                acc = acc_banks.tile([P, CHUNK], F32)
+                acc = acc_banks.tile([P, CHUNK], F32, tag="acc")
                 nc.tensor.matmul_mx(
                     out=acc[:],
                     lhsT=w1_words[:, c * P : (c + 1) * P].bitcast(FP8X4),
@@ -256,29 +279,57 @@ def tile_pairinteractiongrid_pa_t_kernel(tc, p, v, W1, b1, W2, b2, out):
             )
             nc.sync.dma_start(out=out_tiles[k], in_=result[:])
 
-        quantise_inputs()
-        for j in range(AHEAD):
-            pair_tiles[j], steps = batch_steps(j)
-            for step in steps:
-                step()
+        open_batch(0)
+        for w in range(ROUNDS):
+            distances(0, w)
+        for step in vector_steps(0):
+            step()
+        quantise_group(0, 3, distance_of[0])
 
-        rounds_per_batch = LANES * CHUNKS
-        total = BATCHES * rounds_per_batch
+        w1_grouped = keep.tile([P, F_TILES, P, PACK], BF16, align_bytes=64)
+        nc.scalar.copy(out=w1_grouped[:], in_=w1_rows[:].rearrange("q t (i c) -> q c i t", c=F_TILES))
+        w2_grouped = keep.tile([P, D, PACK], BF16, align_bytes=64)
+        nc.scalar.copy(out=w2_grouped[:], in_=w2_rows[:].rearrange("q t d -> q d t"))
+        w1_words = keep.tile([P, F], I32, align_bytes=64)
+        w1_scales = keep.tile([P, F], U8, align_bytes=64)
+        w2_words = keep.tile([P, D], I32, align_bytes=64)
+        w2_scales = keep.tile([P, D], U8, align_bytes=64)
+        nc.vector.quantize_mx(
+            out=w1_words[:].bitcast(FP8X4), scales=w1_scales[:], in_=w1_grouped[:].rearrange("q c i t -> q (c i t)")
+        )
+        nc.vector.quantize_mx(
+            out=w2_words[:].bitcast(FP8X4), scales=w2_scales[:], in_=w2_grouped[:].rearrange("q d t -> q (d t)")
+        )
+
+        open_batch(1)
+        for w in range(ROUNDS):
+            distances(1, w)
+        for step in vector_steps(1):
+            step()
+
+        total = BATCHES * ROUNDS
         steps = []
         for k in range(total + 3):
+            j = k // ROUNDS
+            number = k % ROUNDS
+            if number == 0:
+                steps = []
+                if j + 1 < BATCHES:
+                    steps.append(lambda: quantise_group(j + 1, 3, distance_of[j + 1]))
+                if j + AHEAD < BATCHES:
+                    open_batch(j + AHEAD)
+                    steps.extend(vector_steps(j + AHEAD))
             if 0 <= k - 3 < total:
                 second_layer(k - 3)
             if k < total:
                 first_layer(k)
+            if j + AHEAD < BATCHES:
+                distances(j + AHEAD, number)
             if 0 <= k - 1 < total:
                 regroup(k - 1)
             if 0 <= k - 2 < total:
                 quantise_hidden(k - 2)
             if 0 <= k - 3 < total:
                 finish(k - 3)
-            j = k // rounds_per_batch + AHEAD
-            number = k % rounds_per_batch
-            if number == 0 and j < BATCHES:
-                pair_tiles[j], steps = batch_steps(j)
-            if j < BATCHES and number < len(steps):
+            if number < len(steps):
                 steps[number]()

@@ -29,6 +29,9 @@ F_TILES = F // P
 ROW_TILES = CHUNK // P
 AHEAD = 2
 REPEAT = 4
+REGROUP_LAG = 2
+QUANTISE_LAG = 3
+SECOND_LAG = 5
 SLICE = N // ROUNDS
 
 PLANE = PAIRS // 4
@@ -223,7 +226,7 @@ def tile_pairinteractiongrid_pa_t_kernel(tc, p, v, W1, b1, W2, b2, out):
         def first_layer(k):
             packed = pair_tiles[k // ROUNDS][:, (k % ROUNDS) * CHUNK // PAIRS, :]
             first = k * CHUNK % PAIRS
-            planes = hidden.tile([P, F_TILES, CHUNK], BF16, bufs=4)
+            planes = hidden.tile([P, F_TILES, CHUNK], BF16, bufs=REGROUP_LAG + 3)
             for c in range(F_TILES):
                 acc = acc_banks.tile([P, CHUNK], F32, tag="acc")
                 nc.tensor.matmul_mx(
@@ -247,8 +250,8 @@ def tile_pairinteractiongrid_pa_t_kernel(tc, p, v, W1, b1, W2, b2, out):
             grouped_of[k] = grouped
 
         def quantise_hidden(k):
-            h_words = hidden.tile([P, CHUNK], I32, align_bytes=64)
-            h_scales = hidden.tile([P, CHUNK], U8, align_bytes=64)
+            h_words = hidden.tile([P, CHUNK], I32, bufs=SECOND_LAG - QUANTISE_LAG + 2, align_bytes=64)
+            h_scales = hidden.tile([P, CHUNK], U8, bufs=SECOND_LAG - QUANTISE_LAG + 2, align_bytes=64)
             nc.vector.quantize_mx(
                 out=h_words[:].bitcast(FP8X4), scales=h_scales[:], in_=grouped_of[k][:].rearrange("i w c -> i (w c)")
             )
@@ -309,7 +312,7 @@ def tile_pairinteractiongrid_pa_t_kernel(tc, p, v, W1, b1, W2, b2, out):
 
         total = BATCHES * ROUNDS
         steps = []
-        for k in range(total + 3):
+        for k in range(total + SECOND_LAG):
             j = k // ROUNDS
             number = k % ROUNDS
             if number == 0:
@@ -319,17 +322,17 @@ def tile_pairinteractiongrid_pa_t_kernel(tc, p, v, W1, b1, W2, b2, out):
                 if j + AHEAD < BATCHES:
                     open_batch(j + AHEAD)
                     steps.extend(vector_steps(j + AHEAD))
-            if 0 <= k - 3 < total:
-                second_layer(k - 3)
+            if 0 <= k - SECOND_LAG < total:
+                second_layer(k - SECOND_LAG)
             if k < total:
                 first_layer(k)
             if j + AHEAD < BATCHES:
                 distances(j + AHEAD, number)
-            if 0 <= k - 1 < total:
-                regroup(k - 1)
-            if 0 <= k - 2 < total:
-                quantise_hidden(k - 2)
-            if 0 <= k - 3 < total:
-                finish(k - 3)
+            if 0 <= k - REGROUP_LAG < total:
+                regroup(k - REGROUP_LAG)
+            if 0 <= k - QUANTISE_LAG < total:
+                quantise_hidden(k - QUANTISE_LAG)
+            if 0 <= k - SECOND_LAG < total:
+                finish(k - SECOND_LAG)
             if number < len(steps):
                 steps[number]()

@@ -36,6 +36,9 @@ SLICE = N // ROUNDS
 
 PLANE = PAIRS // 4
 PACKED = PAIRS + PLANE
+V_RUN = 8
+V_WORDS = V_RUN * M
+V_PACKED = V_WORDS + V_WORDS // 4
 
 FLOPS = 2 * GRIDS * PAIRS * (GROUPS * D * F + F * D)
 
@@ -59,6 +62,9 @@ def tile_pairinteractiongrid_pa_t_kernel(tc, p, v, W1, b1, W2, b2, out):
         acc_banks = stack.enter_context(tc.psum_pool(name="acc_banks", bufs=6))
         out_banks = stack.enter_context(tc.psum_pool(name="out_banks", bufs=2))
 
+        identity = keep.tile([P, P], BF16)
+        make_identity(nc, identity[:])
+
         p_rows = keep.tile([P, BATCHES, D], BF16)
         v_rows = keep.tile([P, BATCHES, D], BF16)
         nc.sync.dma_start(out=p_rows[:], in_=p.rearrange("b t n d -> (b t n) d").rearrange("(j r) d -> r j d", r=P))
@@ -66,7 +72,7 @@ def tile_pairinteractiongrid_pa_t_kernel(tc, p, v, W1, b1, W2, b2, out):
         points = keep.tile([P, GRIDS, D], BF16)
         nc.sync.dma_start(out=points[0:N], in_=p.rearrange("b t n d -> n (b t) d"))
         nc.sync.dma_start(out=points[N : N + M], in_=v.rearrange("b t m d -> m (b t) d"))
-        nc.vector.memset(points[N + M :], 0.0)
+        nc.gpsimd.memset(points[N + M :], 0.0)
         w1_rows = keep.tile([P, PACK, F], BF16)
         nc.sync.dma_start(out=w1_rows[:], in_=W1.rearrange("(q t) f -> q t f", t=PACK))
         w2_rows = keep.tile([P, PACK, D], BF16)
@@ -78,18 +84,19 @@ def tile_pairinteractiongrid_pa_t_kernel(tc, p, v, W1, b1, W2, b2, out):
 
         p_packed = keep.tile([P, BATCHES * N * REPEAT + BATCHES * N], I32, align_bytes=64)
         v_packed = keep.tile([P, BATCHES * M + BATCHES * M // 4], I32, align_bytes=64)
-        nc.vector.memset(p_packed[:, BATCHES * N * REPEAT :], 0)
-        nc.vector.memset(v_packed[:, BATCHES * M :], 0)
+        nc.gpsimd.memset(p_packed[:, BATCHES * N * REPEAT :], 0)
+        nc.gpsimd.memset(v_packed[:, BATCHES * M :], 0)
         lane_tiles = []
         for parity in range(2):
             lane_tiles.append(
-                [keep.tile([P, PACKED], I32, name="lane_%d_%d" % (parity, g), align_bytes=64) for g in range(GROUPS)]
+                [
+                    keep.tile([P, V_PACKED if g == 1 else PACKED], I32, name="lane_%d_%d" % (parity, g), align_bytes=64)
+                    for g in range(GROUPS)
+                ]
             )
             for g in (2, 3):
-                nc.vector.memset(lane_tiles[parity][g][:, PAIRS:], 0)
+                nc.gpsimd.memset(lane_tiles[parity][g][:, PAIRS:], 0)
 
-        identity = keep.tile([P, P], BF16)
-        make_identity(nc, identity[:])
         selector = keep.tile([P, N, M], BF16)
         nc.vector.tensor_tensor(
             out=selector[:],
@@ -200,14 +207,27 @@ def tile_pairinteractiongrid_pa_t_kernel(tc, p, v, W1, b1, W2, b2, out):
             lanes = lane_tiles[j % 2][1]
             first = BATCHES * M
             nc.vector.tensor_copy(
-                out=lanes[:, :PAIRS].rearrange("r (n m) -> r n m", m=M),
-                in_=v_packed[:, j * M : (j + 1) * M].unsqueeze(1).to_broadcast([P, N, M]),
+                out=lanes[:, :V_WORDS].rearrange("r (n m) -> r n m", m=M),
+                in_=v_packed[:, j * M : (j + 1) * M].unsqueeze(1).to_broadcast([P, V_RUN, M]),
             )
             nc.vector.tensor_copy(
-                out=lanes[:, PAIRS:].rearrange("r (n s) -> r n s", s=M // 4),
-                in_=v_packed[:, first + j * M // 4 : first + (j + 1) * M // 4].unsqueeze(1).to_broadcast([P, N, M // 4]),
+                out=lanes[:, V_WORDS:].rearrange("r (n s) -> r n s", s=M // 4),
+                in_=v_packed[:, first + j * M // 4 : first + (j + 1) * M // 4]
+                .unsqueeze(1)
+                .to_broadcast([P, V_RUN, M // 4]),
             )
-            to_operand_layout(j, 1)
+            times = N // V_RUN
+            for a in range(LANES):
+                target = pair_tiles[j][QUAD : 2 * QUAD, a, :]
+                source = lanes[a * QUAD : (a + 1) * QUAD, :]
+                nc.sync.dma_start(
+                    out=target[:, :PAIRS].rearrange("r (n w) -> r n w", n=times),
+                    in_=source[:, :V_WORDS].unsqueeze(1).to_broadcast([QUAD, times, V_WORDS]),
+                )
+                nc.sync.dma_start(
+                    out=target[:, PAIRS:].rearrange("r (n w) -> r n w", n=times),
+                    in_=source[:, V_WORDS:].unsqueeze(1).to_broadcast([QUAD, times, V_WORDS // 4]),
+                )
 
         def vector_steps(j):
             return [

@@ -12,6 +12,7 @@ ALU = mybir.AluOpType
 ACT = mybir.ActivationFunctionType
 
 P = 128
+HALVES = 2
 PACK = 4
 QUAD = 32
 GRIDS = 16
@@ -36,9 +37,6 @@ SLICE = N // ROUNDS
 
 PLANE = PAIRS // 4
 PACKED = PAIRS + PLANE
-V_RUN = 8
-V_WORDS = V_RUN * M
-V_PACKED = V_WORDS + V_WORDS // 4
 
 FLOPS = 2 * GRIDS * PAIRS * (GROUPS * D * F + F * D)
 
@@ -90,8 +88,7 @@ def tile_pairinteractiongrid_pa_t_kernel(tc, p, v, W1, b1, W2, b2, out):
         for parity in range(2):
             lane_tiles.append(
                 [
-                    keep.tile([P, V_PACKED if g == 1 else PACKED], I32, name="lane_%d_%d" % (parity, g), align_bytes=64)
-                    for g in range(GROUPS)
+                    keep.tile([P, PACKED], I32, name="lane_%d_%d" % (parity, g), align_bytes=64) for g in range(GROUPS)
                 ]
             )
             for g in (2, 3):
@@ -107,24 +104,30 @@ def tile_pairinteractiongrid_pa_t_kernel(tc, p, v, W1, b1, W2, b2, out):
 
         p_lanes = keep.tile([P, BATCHES, N, REPEAT, PACK], BF16, align_bytes=64)
         v_lanes = keep.tile([P, BATCHES, M, PACK], BF16, align_bytes=64)
-        p_sorted = keep.tile([P, BATCHES, PACK, QUAD], BF16, align_bytes=64)
-        v_sorted = keep.tile([P, BATCHES, PACK, QUAD], BF16, align_bytes=64)
-        p_turned = keep.tile([P, BATCHES, PACK, N], BF16, align_bytes=64)
-        v_turned = keep.tile([P, BATCHES, PACK, M], BF16, align_bytes=64)
-        nc.vector.tensor_copy(out=p_sorted[:], in_=p_rows[:].rearrange("r j (q t) -> r j t q", t=PACK))
-        nc.scalar.copy(out=v_sorted[:], in_=v_rows[:].rearrange("r j (q t) -> r j t q", t=PACK))
-        nc.vector.transpose(
-            out=p_turned[:].rearrange("r j t n -> r (j t n)"), in_=p_sorted[:].rearrange("r j t q -> r (j t q)")
-        )
-        nc.vector.transpose(
-            out=v_turned[:].rearrange("r j t m -> r (j t m)"), in_=v_sorted[:].rearrange("r j t q -> r (j t q)")
-        )
+        p_sorted = keep.tile([P, BATCHES, HALVES, QUAD], F32, align_bytes=64)
+        v_sorted = keep.tile([P, BATCHES, HALVES, QUAD], F32, align_bytes=64)
+        p_turned = keep.tile([P, BATCHES, HALVES, N], F32, align_bytes=64)
+        v_turned = keep.tile([P, BATCHES, HALVES, M], F32, align_bytes=64)
+        for rows, sorted_words, turned in ((p_rows, p_sorted, p_turned), (v_rows, v_sorted, v_turned)):
+            nc.vector.tensor_copy(
+                out=sorted_words[:].bitcast(I32),
+                in_=rows[:].bitcast(I32).rearrange("r j (q u) -> r j u q", u=HALVES),
+            )
+            nc.vector.transpose(
+                out=turned[:].rearrange("r j u n -> r (j u n)"), in_=sorted_words[:].rearrange("r j u q -> r (j u q)")
+            )
         for j in range(BATCHES):
             nc.vector.tensor_copy(
-                out=p_lanes[:, j],
-                in_=p_turned[:, j].rearrange("r t n -> r n t").unsqueeze(2).to_broadcast([P, N, REPEAT, PACK]),
+                out=p_lanes[:, j].bitcast(I32),
+                in_=p_turned[:, j]
+                .bitcast(I32)
+                .rearrange("r u n -> r n u")
+                .unsqueeze(2)
+                .to_broadcast([P, N, REPEAT, HALVES]),
             )
-        nc.scalar.copy(out=v_lanes[:], in_=v_turned[:].rearrange("r j t m -> r j m t"))
+        nc.vector.tensor_copy(
+            out=v_lanes[:].bitcast(I32), in_=v_turned[:].bitcast(I32).rearrange("r j u m -> r j m u")
+        )
         nc.vector.quantize_mx(
             out=words_of(p_packed, 0, BATCHES * N * REPEAT),
             scales=scales_of(p_packed, BATCHES * N * REPEAT, 0, BATCHES * N * REPEAT),
@@ -207,27 +210,14 @@ def tile_pairinteractiongrid_pa_t_kernel(tc, p, v, W1, b1, W2, b2, out):
             lanes = lane_tiles[j % 2][1]
             first = BATCHES * M
             nc.vector.tensor_copy(
-                out=lanes[:, :V_WORDS].rearrange("r (n m) -> r n m", m=M),
-                in_=v_packed[:, j * M : (j + 1) * M].unsqueeze(1).to_broadcast([P, V_RUN, M]),
+                out=lanes[:, :PAIRS].rearrange("r (n m) -> r n m", m=M),
+                in_=v_packed[:, j * M : (j + 1) * M].unsqueeze(1).to_broadcast([P, N, M]),
             )
             nc.vector.tensor_copy(
-                out=lanes[:, V_WORDS:].rearrange("r (n s) -> r n s", s=M // 4),
-                in_=v_packed[:, first + j * M // 4 : first + (j + 1) * M // 4]
-                .unsqueeze(1)
-                .to_broadcast([P, V_RUN, M // 4]),
+                out=lanes[:, PAIRS:].rearrange("r (n s) -> r n s", s=M // 4),
+                in_=v_packed[:, first + j * M // 4 : first + (j + 1) * M // 4].unsqueeze(1).to_broadcast([P, N, M // 4]),
             )
-            times = N // V_RUN
-            for a in range(LANES):
-                target = pair_tiles[j][QUAD : 2 * QUAD, a, :]
-                source = lanes[a * QUAD : (a + 1) * QUAD, :]
-                nc.sync.dma_start(
-                    out=target[:, :PAIRS].rearrange("r (n w) -> r n w", n=times),
-                    in_=source[:, :V_WORDS].unsqueeze(1).to_broadcast([QUAD, times, V_WORDS]),
-                )
-                nc.sync.dma_start(
-                    out=target[:, PAIRS:].rearrange("r (n w) -> r n w", n=times),
-                    in_=source[:, V_WORDS:].unsqueeze(1).to_broadcast([QUAD, times, V_WORDS // 4]),
-                )
+            to_operand_layout(j, 1)
 
         def vector_steps(j):
             return [

@@ -65,12 +65,15 @@ def tile_pairinteractiongrid_pa_t_kernel(tc, p, v, W1, b1, W2, b2, out):
 
         p_rows = keep.tile([P, BATCHES, D], BF16)
         v_rows = keep.tile([P, BATCHES, D], BF16)
+        points = keep.tile([P, GRIDS, D], BF16)
+        by_point = [p.rearrange("b t n d -> n (b t) d"), v.rearrange("b t m d -> m (b t) d")]
+        for side, source in enumerate(by_point):
+            nc.sync.dma_start(out=points[side * N : (side + 1) * N, :LANES], in_=source[:, :LANES])
         nc.sync.dma_start(out=p_rows[:], in_=p.rearrange("b t n d -> (b t n) d").rearrange("(j r) d -> r j d", r=P))
         nc.sync.dma_start(out=v_rows[:], in_=v.rearrange("b t m d -> (b t m) d").rearrange("(j r) d -> r j d", r=P))
-        points = keep.tile([P, GRIDS, D], BF16)
-        nc.sync.dma_start(out=points[0:N], in_=p.rearrange("b t n d -> n (b t) d"))
-        nc.sync.dma_start(out=points[N : N + M], in_=v.rearrange("b t m d -> m (b t) d"))
-        nc.gpsimd.memset(points[N + M :], 0.0)
+        for side, source in enumerate(by_point):
+            nc.sync.dma_start(out=points[side * N : (side + 1) * N, LANES:], in_=source[:, LANES:])
+        nc.vector.memset(points[N + M :], 0.0)
         w1_rows = keep.tile([P, PACK, F], BF16)
         nc.sync.dma_start(out=w1_rows[:], in_=W1.rearrange("(q t) f -> q t f", t=PACK))
         w2_rows = keep.tile([P, PACK, D], BF16)
@@ -82,8 +85,8 @@ def tile_pairinteractiongrid_pa_t_kernel(tc, p, v, W1, b1, W2, b2, out):
 
         p_packed = keep.tile([P, BATCHES * N * REPEAT + BATCHES * N], I32, align_bytes=64)
         v_packed = keep.tile([P, BATCHES * M + BATCHES * M // 4], I32, align_bytes=64)
-        nc.gpsimd.memset(p_packed[:, BATCHES * N * REPEAT :], 0)
-        nc.gpsimd.memset(v_packed[:, BATCHES * M :], 0)
+        nc.vector.memset(p_packed[:, BATCHES * N * REPEAT :], 0)
+        nc.vector.memset(v_packed[:, BATCHES * M :], 0)
         lane_tiles = []
         for parity in range(2):
             lane_tiles.append(
@@ -92,7 +95,7 @@ def tile_pairinteractiongrid_pa_t_kernel(tc, p, v, W1, b1, W2, b2, out):
                 ]
             )
             for g in (2, 3):
-                nc.gpsimd.memset(lane_tiles[parity][g][:, PAIRS:], 0)
+                nc.vector.memset(lane_tiles[parity][g][:, PAIRS:], 0)
 
         selector = keep.tile([P, N, M], BF16)
         nc.vector.tensor_tensor(

@@ -168,9 +168,9 @@ def tile_pairinteractiongrid_pa_t_kernel(tc, p, v, W1, b1, W2, b2, out):
                 func=ACT.Abs,
             )
 
-        def to_operand_layout(j, g):
+        def to_operand_layout(j, g, grids):
             lanes = lane_tiles[j % 2][g]
-            for a in range(LANES):
+            for a in grids:
                 nc.sync.dma_start(
                     out=pair_tiles[j][g * QUAD : (g + 1) * QUAD, a, :], in_=lanes[a * QUAD : (a + 1) * QUAD, :]
                 )
@@ -182,7 +182,10 @@ def tile_pairinteractiongrid_pa_t_kernel(tc, p, v, W1, b1, W2, b2, out):
                 scales=scales_of(lanes, PAIRS, 0, PAIRS),
                 in_=values[:].rearrange("r n m t -> r (n m t)"),
             )
-            to_operand_layout(j, g)
+            to_operand_layout(j, g, grids_at_once(j))
+
+        def grids_at_once(j):
+            return range(LANES) if j > 0 else range(1)
 
         def multiply(j):
             product_of[j] = work.tile([P, N, M, PACK], BF16, name="product", align_bytes=64)
@@ -207,7 +210,7 @@ def tile_pairinteractiongrid_pa_t_kernel(tc, p, v, W1, b1, W2, b2, out):
                 out=lanes[:, PAIRS:].rearrange("r (n s) -> r n s", s=M // 4),
                 in_=p_packed[:, first + j * N : first + (j + 1) * N].unsqueeze(2).to_broadcast([P, N, M // 4]),
             )
-            to_operand_layout(j, 0)
+            to_operand_layout(j, 0, grids_at_once(j))
 
         def repeat_v(j):
             lanes = lane_tiles[j % 2][1]
@@ -220,7 +223,7 @@ def tile_pairinteractiongrid_pa_t_kernel(tc, p, v, W1, b1, W2, b2, out):
                 out=lanes[:, PAIRS:].rearrange("r (n s) -> r n s", s=M // 4),
                 in_=v_packed[:, first + j * M // 4 : first + (j + 1) * M // 4].unsqueeze(1).to_broadcast([P, N, M // 4]),
             )
-            to_operand_layout(j, 1)
+            to_operand_layout(j, 1, grids_at_once(j))
 
         def vector_steps(j):
             return [
@@ -301,6 +304,9 @@ def tile_pairinteractiongrid_pa_t_kernel(tc, p, v, W1, b1, W2, b2, out):
         for step in vector_steps(0):
             step()
         quantise_group(0, 3, distance_of[0])
+        for a in range(1, LANES):
+            for g in range(GROUPS):
+                to_operand_layout(0, g, [a])
 
         w1_grouped = keep.tile([P, F_TILES, P, PACK], BF16, align_bytes=64)
         nc.scalar.copy(out=w1_grouped[:], in_=w1_rows[:].rearrange("q t (i c) -> q c i t", c=F_TILES))

@@ -28,6 +28,7 @@ CHUNK = 512
 ROUNDS = LANES * PAIRS // CHUNK
 F_TILES = F // P
 ROW_TILES = CHUNK // P
+RESULTS = 8
 AHEAD = 2
 REPEAT = 4
 REGROUP_LAG = 2
@@ -289,7 +290,7 @@ def tile_pairinteractiongrid_pa_t_kernel(tc, p, v, W1, b1, W2, b2, out):
             grid_acc_of[k] = grid_acc
 
         def finish(k):
-            result = hidden.tile([P, ROW_TILES, D], F32)
+            result = hidden.tile([P, ROW_TILES, D], F32, bufs=RESULTS)
             nc.vector.tensor_tensor(
                 out=result[:],
                 in0=grid_acc_of[k][:],

@@ -33,7 +33,7 @@ AHEAD = 2
 REPEAT = 4
 REGROUP_LAG = 2
 QUANTISE_LAG = 3
-SECOND_LAG = 5
+SECOND_LAG = 4
 SLICE = N // ROUNDS
 
 PLANE = PAIRS // 4
@@ -234,6 +234,8 @@ def tile_pairinteractiongrid_pa_t_kernel(tc, p, v, W1, b1, W2, b2, out):
                 lambda: quantise_group(j, 2, product_of[j]),
             ]
 
+        total = BATCHES * ROUNDS
+
         out_tiles = out.rearrange("b t (h s r) d -> (b t h) r s d", s=ROW_TILES, r=P)
         planes_of = {}
         grouped_of = {}
@@ -260,7 +262,8 @@ def tile_pairinteractiongrid_pa_t_kernel(tc, p, v, W1, b1, W2, b2, out):
 
         def regroup(k):
             grouped = hidden.tile([P, CHUNK, PACK], BF16, align_bytes=64)
-            nc.vector.tensor_copy(
+            copy = nc.scalar.copy if k == total - 1 else nc.vector.tensor_copy
+            copy(
                 out=grouped[:].rearrange("i (w e) c -> i w c e", e=4),
                 in_=planes_of[k][:].rearrange("i c (w e) -> i w c e", e=4),
             )
@@ -291,13 +294,15 @@ def tile_pairinteractiongrid_pa_t_kernel(tc, p, v, W1, b1, W2, b2, out):
 
         def finish(k):
             result = hidden.tile([P, ROW_TILES, D], F32, bufs=RESULTS)
-            nc.vector.tensor_tensor(
-                out=result[:],
-                in0=grid_acc_of[k][:],
-                in1=b2_rows[:].unsqueeze(1).to_broadcast([P, ROW_TILES, D]),
-                op=ALU.add,
-            )
-            nc.sync.dma_start(out=out_tiles[k], in_=result[:])
+            count = ROW_TILES // 2 if k == total - 1 else ROW_TILES
+            for s in range(0, ROW_TILES, count):
+                nc.vector.tensor_tensor(
+                    out=result[:, s : s + count],
+                    in0=grid_acc_of[k][:, s : s + count],
+                    in1=b2_rows[:].unsqueeze(1).to_broadcast([P, count, D]),
+                    op=ALU.add,
+                )
+                nc.sync.dma_start(out=out_tiles[k][:, s : s + count], in_=result[:, s : s + count])
 
         open_batch(0)
         for w in range(ROUNDS):
@@ -330,7 +335,6 @@ def tile_pairinteractiongrid_pa_t_kernel(tc, p, v, W1, b1, W2, b2, out):
         for step in vector_steps(1):
             step()
 
-        total = BATCHES * ROUNDS
         steps = []
         for k in range(total + SECOND_LAG):
             j = k // ROUNDS
@@ -354,5 +358,6 @@ def tile_pairinteractiongrid_pa_t_kernel(tc, p, v, W1, b1, W2, b2, out):
                 quantise_hidden(k - QUANTISE_LAG)
             if 0 <= k - SECOND_LAG < total:
                 finish(k - SECOND_LAG)
-            if number < len(steps):
-                steps[number]()
+            for i, step in enumerate(steps):
+                if number == i * ROUNDS // len(steps):
+                    step()

@@ -38,6 +38,9 @@ SLICE = N // ROUNDS
 
 PLANE = PAIRS // 4
 PACKED = PAIRS + PLANE
+V_RUN = 8
+V_WORDS = V_RUN * M
+V_PACKED = V_WORDS + V_WORDS // 4
 
 FLOPS = 2 * GRIDS * PAIRS * (GROUPS * D * F + F * D)
 
@@ -92,7 +95,8 @@ def tile_pairinteractiongrid_pa_t_kernel(tc, p, v, W1, b1, W2, b2, out):
         for parity in range(2):
             lane_tiles.append(
                 [
-                    keep.tile([P, PACKED], I32, name="lane_%d_%d" % (parity, g), align_bytes=64) for g in range(GROUPS)
+                    keep.tile([P, V_PACKED if g == 1 else PACKED], I32, name="lane_%d_%d" % (parity, g), align_bytes=256)
+                    for g in range(GROUPS)
                 ]
             )
             for g in (2, 3):
@@ -148,7 +152,7 @@ def tile_pairinteractiongrid_pa_t_kernel(tc, p, v, W1, b1, W2, b2, out):
         product_of = {}
 
         def open_batch(j):
-            pair_tiles[j] = operands.tile([P, LANES, PACKED], I32, name="pair_mx", align_bytes=64)
+            pair_tiles[j] = operands.tile([P, LANES, PACKED], I32, name="pair_mx", align_bytes=256)
             distance_of[j] = work.tile([P, N, M, PACK], BF16, name="distance", align_bytes=64)
 
         def distances(j, w):
@@ -172,9 +176,16 @@ def tile_pairinteractiongrid_pa_t_kernel(tc, p, v, W1, b1, W2, b2, out):
         def to_operand_layout(j, g, grids):
             lanes = lane_tiles[j % 2][g]
             for a in grids:
-                nc.sync.dma_start(
-                    out=pair_tiles[j][g * QUAD : (g + 1) * QUAD, a, :], in_=lanes[a * QUAD : (a + 1) * QUAD, :]
-                )
+                target = pair_tiles[j][g * QUAD : (g + 1) * QUAD, a, :]
+                source = lanes[a * QUAD : (a + 1) * QUAD, :]
+                if g != 1:
+                    nc.sync.dma_start(out=target, in_=source)
+                    continue
+                for old, new in ((slice(0, V_WORDS), slice(0, PAIRS)), (slice(V_WORDS, V_PACKED), slice(PAIRS, PACKED))):
+                    nc.sync.dma_start(
+                        out=target[:, new].rearrange("r (n w) -> r n w", n=N // V_RUN),
+                        in_=source[:, old].unsqueeze(1).to_broadcast([QUAD, N // V_RUN, old.stop - old.start]),
+                    )
 
         def quantise_group(j, g, values):
             lanes = lane_tiles[j % 2][g]
@@ -217,12 +228,14 @@ def tile_pairinteractiongrid_pa_t_kernel(tc, p, v, W1, b1, W2, b2, out):
             lanes = lane_tiles[j % 2][1]
             first = BATCHES * M
             nc.vector.tensor_copy(
-                out=lanes[:, :PAIRS].rearrange("r (n m) -> r n m", m=M),
-                in_=v_packed[:, j * M : (j + 1) * M].unsqueeze(1).to_broadcast([P, N, M]),
+                out=lanes[:, :V_WORDS].rearrange("r (n m) -> r n m", m=M),
+                in_=v_packed[:, j * M : (j + 1) * M].unsqueeze(1).to_broadcast([P, V_RUN, M]),
             )
             nc.vector.tensor_copy(
-                out=lanes[:, PAIRS:].rearrange("r (n s) -> r n s", s=M // 4),
-                in_=v_packed[:, first + j * M // 4 : first + (j + 1) * M // 4].unsqueeze(1).to_broadcast([P, N, M // 4]),
+                out=lanes[:, V_WORDS:].rearrange("r (n s) -> r n s", s=M // 4),
+                in_=v_packed[:, first + j * M // 4 : first + (j + 1) * M // 4]
+                .unsqueeze(1)
+                .to_broadcast([P, V_RUN, M // 4]),
             )
             to_operand_layout(j, 1, grids_at_once(j))
 

@@ -277,8 +277,8 @@ def tile_pairinteractiongrid_pa_t_kernel(tc, p, v, W1, b1, W2, b2, out):
             grouped = hidden.tile([P, CHUNK, PACK], BF16, align_bytes=64)
             copy = nc.scalar.copy if k == total - 1 else nc.vector.tensor_copy
             copy(
-                out=grouped[:].rearrange("i (w e) c -> i w c e", e=4),
-                in_=planes_of[k][:].rearrange("i c (w e) -> i w c e", e=4),
+                out=grouped[:].rearrange("i (w e) (h l) -> i w h e l", e=4, l=2),
+                in_=planes_of[k][:].rearrange("i (h l) (w e) -> i w h e l", e=4, l=2),
             )
             grouped_of[k] = grouped
 

@@ -34,7 +34,8 @@ REPEAT = 4
 REGROUP_LAG = 2
 QUANTISE_LAG = 3
 SECOND_LAG = 4
-SLICE = N // ROUNDS
+SLICES = 4
+SLICE = N // SLICES
 
 PLANE = PAIRS // 4
 PACKED = PAIRS + PLANE
@@ -116,15 +117,20 @@ def tile_pairinteractiongrid_pa_t_kernel(tc, p, v, W1, b1, W2, b2, out):
         v_sorted = keep.tile([P, BATCHES, HALVES, QUAD], F32, align_bytes=64)
         p_turned = keep.tile([P, BATCHES, HALVES, N], F32, align_bytes=64)
         v_turned = keep.tile([P, BATCHES, HALVES, M], F32, align_bytes=64)
-        for rows, sorted_words, turned in ((p_rows, p_sorted, p_turned), (v_rows, v_sorted, v_turned)):
+        for rows, sorted_words in ((v_rows, v_sorted), (p_rows, p_sorted)):
             nc.vector.tensor_copy(
                 out=sorted_words[:].bitcast(I32),
                 in_=rows[:].bitcast(I32).rearrange("r j (q u) -> r j u q", u=HALVES),
             )
+        for sorted_words, turned in ((v_sorted, v_turned), (p_sorted, p_turned)):
             nc.vector.transpose(
                 out=turned[:].rearrange("r j u n -> r (j u n)"), in_=sorted_words[:].rearrange("r j u q -> r (j u q)")
             )
-        for j in range(BATCHES):
+        nc.vector.tensor_copy(
+            out=v_lanes[:].bitcast(I32), in_=v_turned[:].bitcast(I32).rearrange("r j u m -> r j m u")
+        )
+
+        def lane_points(j):
             nc.vector.tensor_copy(
                 out=p_lanes[:, j].bitcast(I32),
                 in_=p_turned[:, j]
@@ -133,19 +139,20 @@ def tile_pairinteractiongrid_pa_t_kernel(tc, p, v, W1, b1, W2, b2, out):
                 .unsqueeze(2)
                 .to_broadcast([P, N, REPEAT, HALVES]),
             )
-        nc.vector.tensor_copy(
-            out=v_lanes[:].bitcast(I32), in_=v_turned[:].bitcast(I32).rearrange("r j u m -> r j m u")
-        )
-        nc.vector.quantize_mx(
-            out=words_of(p_packed, 0, BATCHES * N * REPEAT),
-            scales=scales_of(p_packed, BATCHES * N * REPEAT, 0, BATCHES * N * REPEAT),
-            in_=p_lanes[:].rearrange("r j n e t -> r (j n e t)"),
-        )
-        nc.vector.quantize_mx(
-            out=words_of(v_packed, 0, BATCHES * M),
-            scales=scales_of(v_packed, BATCHES * M, 0, BATCHES * M),
-            in_=v_lanes[:].rearrange("r j m t -> r (j m t)"),
-        )
+
+        def quantise_p(j):
+            nc.vector.quantize_mx(
+                out=words_of(p_packed, j * N * REPEAT, N * REPEAT),
+                scales=scales_of(p_packed, BATCHES * N * REPEAT, j * N * REPEAT, N * REPEAT),
+                in_=p_lanes[:, j].rearrange("r n e t -> r (n e t)"),
+            )
+
+        def quantise_v():
+            nc.vector.quantize_mx(
+                out=words_of(v_packed, 0, BATCHES * M),
+                scales=scales_of(v_packed, BATCHES * M, 0, BATCHES * M),
+                in_=v_lanes[:].rearrange("r j m t -> r (j m t)"),
+            )
 
         pair_tiles = {}
         distance_of = {}
@@ -158,7 +165,7 @@ def tile_pairinteractiongrid_pa_t_kernel(tc, p, v, W1, b1, W2, b2, out):
         def distances(j, w):
             some = slice(w * SLICE, (w + 1) * SLICE)
             by_feature = points[:, j * LANES : (j + 1) * LANES, :].rearrange("k a (q t) -> k t (a q)", t=PACK)
-            bank = acc_banks.tile([P, PACK, SLICE * M], F32, tag="acc")
+            bank = acc_banks.tile([P, PACK, SLICE * M], BF16, tag="acc")
             for t in range(PACK):
                 nc.tensor.matmul(
                     out=bank[:, t, :],
@@ -318,19 +325,41 @@ def tile_pairinteractiongrid_pa_t_kernel(tc, p, v, W1, b1, W2, b2, out):
                 nc.sync.dma_start(out=out_tiles[k][:, s : s + count], in_=result[:, s : s + count])
 
         open_batch(0)
-        for w in range(ROUNDS):
+        for w in range(SLICES):
             distances(0, w)
-        for step in vector_steps(0):
+        lane_points(0)
+        lane_points(1)
+        multiply(0)
+        quantise_p(0)
+        quantise_v()
+        for step in vector_steps(0)[1:]:
             step()
         quantise_group(0, 3, distance_of[0])
         for a in range(1, LANES):
             for g in range(GROUPS):
                 to_operand_layout(0, g, [a])
 
+        lane_points(2)
+        lane_points(3)
+        for j in range(1, BATCHES):
+            quantise_p(j)
+
         w1_grouped = keep.tile([P, F_TILES, P, PACK], BF16, align_bytes=64)
-        nc.scalar.copy(out=w1_grouped[:], in_=w1_rows[:].rearrange("q t (i c) -> q c i t", c=F_TILES))
         w2_grouped = keep.tile([P, D, PACK], BF16, align_bytes=64)
-        nc.scalar.copy(out=w2_grouped[:], in_=w2_rows[:].rearrange("q t d -> q d t"))
+        by_unit = w1_rows[:].rearrange("q t (i c) -> q c i t", c=F_TILES)
+        for pair in range(0, F_TILES, 2):
+            bank = acc_banks.tile([P, 2, P, PACK], BF16, tag="acc")
+            for c in range(2):
+                nc.tensor.matmul(out=bank[:, c], lhsT=identity[:], rhs=by_unit[:, pair + c], start=True, stop=True)
+            nc.scalar.copy(
+                out=w1_grouped[:, pair : pair + 2].rearrange("q c i t -> q (c i t)"),
+                in_=bank[:].rearrange("q c i t -> q (c i t)"),
+            )
+        bank = acc_banks.tile([P, D, PACK], BF16, tag="acc")
+        nc.tensor.matmul(
+            out=bank[:], lhsT=identity[:], rhs=w2_rows[:].rearrange("q t d -> q d t"), start=True, stop=True
+        )
+        nc.scalar.copy(out=w2_grouped[:].rearrange("q d t -> q (d t)"), in_=bank[:].rearrange("q d t -> q (d t)"))
         w1_words = keep.tile([P, F], I32, align_bytes=64)
         w1_scales = keep.tile([P, F], U8, align_bytes=64)
         w2_words = keep.tile([P, D], I32, align_bytes=64)
@@ -343,7 +372,7 @@ def tile_pairinteractiongrid_pa_t_kernel(tc, p, v, W1, b1, W2, b2, out):
         )
 
         open_batch(1)
-        for w in range(ROUNDS):
+        for w in range(SLICES):
             distances(1, w)
         for step in vector_steps(1):
             step()
@@ -363,8 +392,8 @@ def tile_pairinteractiongrid_pa_t_kernel(tc, p, v, W1, b1, W2, b2, out):
                 second_layer(k - SECOND_LAG)
             if k < total:
                 first_layer(k)
-            if j + AHEAD < BATCHES:
-                distances(j + AHEAD, number)
+            if j + AHEAD < BATCHES and number % (ROUNDS // SLICES) == 0:
+                distances(j + AHEAD, number * SLICES // ROUNDS)
             if 0 <= k - REGROUP_LAG < total:
                 regroup(k - REGROUP_LAG)
             if 0 <= k - QUANTISE_LAG < total:

from contextlib import ExitStack

import concourse.mybir as mybir
from concourse.masks import make_identity

BF16 = mybir.dt.bfloat16
F32 = mybir.dt.float32
I32 = mybir.dt.int32
U8 = mybir.dt.uint8
FP8X4 = mybir.dt.float8_e4m3fn_x4
ALU = mybir.AluOpType
ACT = mybir.ActivationFunctionType

P = 128
HALVES = 2
PACK = 4
QUAD = 32
GRIDS = 16
N = 32
M = 32
D = 128
F = 512
GROUPS = 4
LANES = 4
BATCHES = GRIDS // LANES
PAIRS = N * M
CHUNK = 512
ROUNDS = LANES * PAIRS // CHUNK
F_TILES = F // P
ROW_TILES = CHUNK // P
RESULTS = 8
AHEAD = 2
REPEAT = 4
REGROUP_LAG = 2
QUANTISE_LAG = 3
SECOND_LAG = 4
SLICES = 4
SLICE = N // SLICES

PLANE = PAIRS // 4
PACKED = PAIRS + PLANE
V_RUN = 8
V_WORDS = V_RUN * M
V_PACKED = V_WORDS + V_WORDS // 4

FLOPS = 2 * GRIDS * PAIRS * (GROUPS * D * F + F * D)


def words_of(packed, first, count):
    return packed[:, first : first + count].bitcast(FP8X4)


def scales_of(packed, words, first, count):
    return packed[:, words + first // 4 : words + (first + count) // 4].bitcast(U8)


def tile_pairinteractiongrid_pa_t_kernel(tc, p, v, W1, b1, W2, b2, out):
    nc = tc.nc
    with ExitStack() as stack:
        stack.enter_context(tc.manual_schedule())
        keep = stack.enter_context(tc.tile_pool(name="keep", bufs=1))
        work = stack.enter_context(tc.tile_pool(name="work", bufs=2))
        operands = stack.enter_context(tc.tile_pool(name="operands", bufs=AHEAD + 1))
        hidden = stack.enter_context(tc.tile_pool(name="hidden", bufs=3))
        acc_banks = stack.enter_context(tc.psum_pool(name="acc_banks", bufs=6))
        out_banks = stack.enter_context(tc.psum_pool(name="out_banks", bufs=2))

        identity = keep.tile([P, P], BF16)
        make_identity(nc, identity[:])

        p_rows = keep.tile([P, BATCHES, D], BF16)
        v_rows = keep.tile([P, BATCHES, D], BF16)
        points = keep.tile([P, GRIDS, D], BF16)
        by_point = [p.rearrange("b t n d -> n (b t) d"), v.rearrange("b t m d -> m (b t) d")]
        for side, source in enumerate(by_point):
            nc.sync.dma_start(out=points[side * N : (side + 1) * N, :LANES], in_=source[:, :LANES])
        nc.sync.dma_start(out=p_rows[:], in_=p.rearrange("b t n d -> (b t n) d").rearrange("(j r) d -> r j d", r=P))
        nc.sync.dma_start(out=v_rows[:], in_=v.rearrange("b t m d -> (b t m) d").rearrange("(j r) d -> r j d", r=P))
        for side, source in enumerate(by_point):
            nc.sync.dma_start(out=points[side * N : (side + 1) * N, LANES:], in_=source[:, LANES:])
        nc.vector.memset(points[N + M :], 0.0)
        w1_rows = keep.tile([P, PACK, F], BF16)
        nc.sync.dma_start(out=w1_rows[:], in_=W1.rearrange("(q t) f -> q t f", t=PACK))
        w2_rows = keep.tile([P, PACK, D], BF16)
        nc.sync.dma_start(out=w2_rows[:], in_=W2.rearrange("(q t) d -> q t d", t=PACK))
        b1_cols = keep.tile([P, F_TILES], BF16)
        nc.sync.dma_start(out=b1_cols[:], in_=b1.rearrange("(i c) -> i c", c=F_TILES))
        b2_rows = keep.tile([P, D], BF16)
        nc.sync.dma_start(out=b2_rows[:], in_=b2.partition_broadcast(P))

        p_packed = keep.tile([P, BATCHES * N * REPEAT + BATCHES * N], I32, align_bytes=64)
        v_packed = keep.tile([P, BATCHES * M + BATCHES * M // 4], I32, align_bytes=64)
        nc.vector.memset(p_packed[:, BATCHES * N * REPEAT :], 0)
        nc.vector.memset(v_packed[:, BATCHES * M :], 0)
        lane_tiles = []
        for parity in range(2):
            lane_tiles.append(
                [
                    keep.tile([P, V_PACKED if g == 1 else PACKED], I32, name="lane_%d_%d" % (parity, g), align_bytes=256)
                    for g in range(GROUPS)
                ]
            )
            for g in (2, 3):
                nc.vector.memset(lane_tiles[parity][g][:, PAIRS:], 0)

        selector = keep.tile([P, N, M], BF16)
        nc.vector.tensor_tensor(
            out=selector[:],
            in0=identity[:, 0:N].unsqueeze(2).to_broadcast([P, N, M]),
            in1=identity[:, N : N + M].unsqueeze(1).to_broadcast([P, N, M]),
            op=ALU.subtract,
        )

        p_lanes = keep.tile([P, BATCHES, N, REPEAT, PACK], BF16, align_bytes=64)
        v_lanes = keep.tile([P, BATCHES, M, PACK], BF16, align_bytes=64)
        p_sorted = keep.tile([P, BATCHES, HALVES, QUAD], F32, align_bytes=64)
        v_sorted = keep.tile([P, BATCHES, HALVES, QUAD], F32, align_bytes=64)
        p_turned = keep.tile([P, BATCHES, HALVES, N], F32, align_bytes=64)
        v_turned = keep.tile([P, BATCHES, HALVES, M], F32, align_bytes=64)
        for rows, sorted_words in ((v_rows, v_sorted), (p_rows, p_sorted)):
            nc.vector.tensor_copy(
                out=sorted_words[:].bitcast(I32),
                in_=rows[:].bitcast(I32).rearrange("r j (q u) -> r j u q", u=HALVES),
            )
        for sorted_words, turned in ((v_sorted, v_turned), (p_sorted, p_turned)):
            nc.vector.transpose(
                out=turned[:].rearrange("r j u n -> r (j u n)"), in_=sorted_words[:].rearrange("r j u q -> r (j u q)")
            )
        nc.vector.tensor_copy(
            out=v_lanes[:].bitcast(I32), in_=v_turned[:].bitcast(I32).rearrange("r j u m -> r j m u")
        )

        def lane_points(j):
            nc.vector.tensor_copy(
                out=p_lanes[:, j].bitcast(I32),
                in_=p_turned[:, j]
                .bitcast(I32)
                .rearrange("r u n -> r n u")
                .unsqueeze(2)
                .to_broadcast([P, N, REPEAT, HALVES]),
            )

        def quantise_p(j):
            nc.vector.quantize_mx(
                out=words_of(p_packed, j * N * REPEAT, N * REPEAT),
                scales=scales_of(p_packed, BATCHES * N * REPEAT, j * N * REPEAT, N * REPEAT),
                in_=p_lanes[:, j].rearrange("r n e t -> r (n e t)"),
            )

        def quantise_v():
            nc.vector.quantize_mx(
                out=words_of(v_packed, 0, BATCHES * M),
                scales=scales_of(v_packed, BATCHES * M, 0, BATCHES * M),
                in_=v_lanes[:].rearrange("r j m t -> r (j m t)"),
            )

        pair_tiles = {}
        distance_of = {}
        product_of = {}

        def open_batch(j):
            pair_tiles[j] = operands.tile([P, LANES, PACKED], I32, name="pair_mx", align_bytes=256)
            distance_of[j] = work.tile([P, N, M, PACK], BF16, name="distance", align_bytes=64)

        def distances(j, w):
            some = slice(w * SLICE, (w + 1) * SLICE)
            by_feature = points[:, j * LANES : (j + 1) * LANES, :].rearrange("k a (q t) -> k t (a q)", t=PACK)
            bank = acc_banks.tile([P, PACK, SLICE * M], BF16, tag="acc")
            for t in range(PACK):
                nc.tensor.matmul(
                    out=bank[:, t, :],
                    lhsT=by_feature[:, t, :],
                    rhs=selector[:, some, :].rearrange("k n m -> k (n m)"),
                    start=True,
                    stop=True,
                )
            nc.scalar.activation(
                out=distance_of[j][:, some].rearrange("r n m t -> r (n m) t"),
                in_=bank[:].rearrange("r t w -> r w t"),
                func=ACT.Abs,
            )

        def to_operand_layout(j, g, grids):
            lanes = lane_tiles[j % 2][g]
            for a in grids:
                target = pair_tiles[j][g * QUAD : (g + 1) * QUAD, a, :]
                source = lanes[a * QUAD : (a + 1) * QUAD, :]
                if g != 1:
                    nc.sync.dma_start(out=target, in_=source)
                    continue
                for old, new in ((slice(0, V_WORDS), slice(0, PAIRS)), (slice(V_WORDS, V_PACKED), slice(PAIRS, PACKED))):
                    nc.sync.dma_start(
                        out=target[:, new].rearrange("r (n w) -> r n w", n=N // V_RUN),
                        in_=source[:, old].unsqueeze(1).to_broadcast([QUAD, N // V_RUN, old.stop - old.start]),
                    )

        def quantise_group(j, g, values):
            lanes = lane_tiles[j % 2][g]
            nc.vector.quantize_mx(
                out=words_of(lanes, 0, PAIRS),
                scales=scales_of(lanes, PAIRS, 0, PAIRS),
                in_=values[:].rearrange("r n m t -> r (n m t)"),
            )
            to_operand_layout(j, g, grids_at_once(j))

        def grids_at_once(j):
            return range(LANES) if j > 0 else range(1)

        def multiply(j):
            product_of[j] = work.tile([P, N, M, PACK], BF16, name="product", align_bytes=64)
            nc.vector.tensor_tensor(
                out=product_of[j][:],
                in0=p_lanes[:, j, :, 0, :].unsqueeze(2).to_broadcast([P, N, M, PACK]),
                in1=v_lanes[:, j].unsqueeze(1).to_broadcast([P, N, M, PACK]),
                op=ALU.mult,
            )

        def repeat_p(j):
            lanes = lane_tiles[j % 2][0]
            first = BATCHES * N * REPEAT
            nc.vector.tensor_copy(
                out=lanes[:, :PAIRS].rearrange("r (n s e) -> r n s e", s=M // REPEAT, e=REPEAT),
                in_=p_packed[:, j * N * REPEAT : (j + 1) * N * REPEAT]
                .rearrange("r (n e) -> r n e", e=REPEAT)
                .unsqueeze(2)
                .to_broadcast([P, N, M // REPEAT, REPEAT]),
            )
            nc.vector.tensor_copy(
                out=lanes[:, PAIRS:].rearrange("r (n s) -> r n s", s=M // 4),
                in_=p_packed[:, first + j * N : first + (j + 1) * N].unsqueeze(2).to_broadcast([P, N, M // 4]),
            )
            to_operand_layout(j, 0, grids_at_once(j))

        def repeat_v(j):
            lanes = lane_tiles[j % 2][1]
            first = BATCHES * M
            nc.vector.tensor_copy(
                out=lanes[:, :V_WORDS].rearrange("r (n m) -> r n m", m=M),
                in_=v_packed[:, j * M : (j + 1) * M].unsqueeze(1).to_broadcast([P, V_RUN, M]),
            )
            nc.vector.tensor_copy(
                out=lanes[:, V_WORDS:].rearrange("r (n s) -> r n s", s=M // 4),
                in_=v_packed[:, first + j * M // 4 : first + (j + 1) * M // 4]
                .unsqueeze(1)
                .to_broadcast([P, V_RUN, M // 4]),
            )
            to_operand_layout(j, 1, grids_at_once(j))

        def vector_steps(j):
            return [
                lambda: multiply(j),
                lambda: repeat_p(j),
                lambda: repeat_v(j),
                lambda: quantise_group(j, 2, product_of[j]),
            ]

        total = BATCHES * ROUNDS

        out_tiles = out.rearrange("b t (h s r) d -> (b t h) r s d", s=ROW_TILES, r=P)
        planes_of = {}
        grouped_of = {}
        hidden_mx_of = {}
        grid_acc_of = {}

        def first_layer(k):
            packed = pair_tiles[k // ROUNDS][:, (k % ROUNDS) * CHUNK // PAIRS, :]
            first = k * CHUNK % PAIRS
            planes = hidden.tile([P, F_TILES, CHUNK], BF16, bufs=REGROUP_LAG + 3)
            for c in range(F_TILES):
                acc = acc_banks.tile([P, CHUNK], F32, tag="acc")
                nc.tensor.matmul_mx(
                    out=acc[:],
                    lhsT=w1_words[:, c * P : (c + 1) * P].bitcast(FP8X4),
                    lhsT_scale=w1_scales[:, c * P : (c + 1) * P],
                    rhs=words_of(packed, first, CHUNK),
                    rhs_scale=scales_of(packed, PAIRS, first, CHUNK),
                    start=True,
                    stop=True,
                )
                nc.scalar.activation(out=planes[:, c, :], in_=acc[:], func=ACT.Silu, bias=b1_cols[:, c : c + 1])
            planes_of[k] = planes

        def regroup(k):
            grouped = hidden.tile([P, CHUNK, PACK], BF16, align_bytes=64)
            copy = nc.scalar.copy if k == total - 1 else nc.vector.tensor_copy
            copy(
                out=grouped[:].rearrange("i (w e) (h l) -> i w h e l", e=4, l=2),
                in_=planes_of[k][:].rearrange("i (h l) (w e) -> i w h e l", e=4, l=2),
            )
            grouped_of[k] = grouped

        def quantise_hidden(k):
            h_words = hidden.tile([P, CHUNK], I32, bufs=SECOND_LAG - QUANTISE_LAG + 2, align_bytes=64)
            h_scales = hidden.tile([P, CHUNK], U8, bufs=SECOND_LAG - QUANTISE_LAG + 2, align_bytes=64)
            nc.vector.quantize_mx(
                out=h_words[:].bitcast(FP8X4), scales=h_scales[:], in_=grouped_of[k][:].rearrange("i w c -> i (w c)")
            )
            hidden_mx_of[k] = (h_words, h_scales)

        def second_layer(k):
            h_words, h_scales = hidden_mx_of[k]
            grid_acc = out_banks.tile([P, ROW_TILES, D], F32)
            for s in range(ROW_TILES):
                nc.tensor.matmul_mx(
                    out=grid_acc[:, s, :],
                    lhsT=h_words[:, s * P : (s + 1) * P].bitcast(FP8X4),
                    lhsT_scale=h_scales[:, s * P : (s + 1) * P],
                    rhs=w2_words[:].bitcast(FP8X4),
                    rhs_scale=w2_scales[:],
                    start=True,
                    stop=True,
                )
            grid_acc_of[k] = grid_acc

        def finish(k):
            result = hidden.tile([P, ROW_TILES, D], F32, bufs=RESULTS)
            count = ROW_TILES // 2 if k == total - 1 else ROW_TILES
            for s in range(0, ROW_TILES, count):
                nc.vector.tensor_tensor(
                    out=result[:, s : s + count],
                    in0=grid_acc_of[k][:, s : s + count],
                    in1=b2_rows[:].unsqueeze(1).to_broadcast([P, count, D]),
                    op=ALU.add,
                )
                nc.sync.dma_start(out=out_tiles[k][:, s : s + count], in_=result[:, s : s + count])

        open_batch(0)
        for w in range(SLICES):
            distances(0, w)
        lane_points(0)
        lane_points(1)
        multiply(0)
        quantise_p(0)
        quantise_v()
        for step in vector_steps(0)[1:]:
            step()
        quantise_group(0, 3, distance_of[0])
        for a in range(1, LANES):
            for g in range(GROUPS):
                to_operand_layout(0, g, [a])

        lane_points(2)
        lane_points(3)
        for j in range(1, BATCHES):
            quantise_p(j)

        w1_grouped = keep.tile([P, F_TILES, P, PACK], BF16, align_bytes=64)
        w2_grouped = keep.tile([P, D, PACK], BF16, align_bytes=64)
        by_unit = w1_rows[:].rearrange("q t (i c) -> q c i t", c=F_TILES)
        for pair in range(0, F_TILES, 2):
            bank = acc_banks.tile([P, 2, P, PACK], BF16, tag="acc")
            for c in range(2):
                nc.tensor.matmul(out=bank[:, c], lhsT=identity[:], rhs=by_unit[:, pair + c], start=True, stop=True)
            nc.scalar.copy(
                out=w1_grouped[:, pair : pair + 2].rearrange("q c i t -> q (c i t)"),
                in_=bank[:].rearrange("q c i t -> q (c i t)"),
            )
        bank = acc_banks.tile([P, D, PACK], BF16, tag="acc")
        nc.tensor.matmul(
            out=bank[:], lhsT=identity[:], rhs=w2_rows[:].rearrange("q t d -> q d t"), start=True, stop=True
        )
        nc.scalar.copy(out=w2_grouped[:].rearrange("q d t -> q (d t)"), in_=bank[:].rearrange("q d t -> q (d t)"))
        w1_words = keep.tile([P, F], I32, align_bytes=64)
        w1_scales = keep.tile([P, F], U8, align_bytes=64)
        w2_words = keep.tile([P, D], I32, align_bytes=64)
        w2_scales = keep.tile([P, D], U8, align_bytes=64)
        nc.vector.quantize_mx(
            out=w1_words[:].bitcast(FP8X4), scales=w1_scales[:], in_=w1_grouped[:].rearrange("q c i t -> q (c i t)")
        )
        nc.vector.quantize_mx(
            out=w2_words[:].bitcast(FP8X4), scales=w2_scales[:], in_=w2_grouped[:].rearrange("q d t -> q (d t)")
        )

        open_batch(1)
        for w in range(SLICES):
            distances(1, w)
        for step in vector_steps(1):
            step()

        steps = []
        for k in range(total + SECOND_LAG):
            j = k // ROUNDS
            number = k % ROUNDS
            if number == 0:
                steps = []
                if j + 1 < BATCHES:
                    steps.append(lambda: quantise_group(j + 1, 3, distance_of[j + 1]))
                if j + AHEAD < BATCHES:
                    open_batch(j + AHEAD)
                    steps.extend(vector_steps(j + AHEAD))
            if 0 <= k - SECOND_LAG < total:
                second_layer(k - SECOND_LAG)
            if k < total:
                first_layer(k)
            if j + AHEAD < BATCHES and number % (ROUNDS // SLICES) == 0:
                distances(j + AHEAD, number * SLICES // ROUNDS)
            if 0 <= k - REGROUP_LAG < total:
                regroup(k - REGROUP_LAG)
            if 0 <= k - QUANTISE_LAG < total:
                quantise_hidden(k - QUANTISE_LAG)
            if 0 <= k - SECOND_LAG < total:
                finish(k - SECOND_LAG)
            for i, step in enumerate(steps):
                if number == i * ROUNDS // len(steps):
                    step()
